import numpy as np
import ml_dtypes


def mxq(x, axis, fmt="e4m3"):
    dtype, down = {"e4m3": (ml_dtypes.float8_e4m3fn, 7), "e5m2": (ml_dtypes.float8_e5m2, 14)}[fmt]
    v = np.moveaxis(np.asarray(x, np.float32).astype(ml_dtypes.bfloat16).astype(np.float64), axis, -1)
    blocks = v.reshape(v.shape[:-1] + (-1, 32))
    amax = np.abs(blocks).max(-1, keepdims=True)
    byte = np.maximum(np.where(amax > 0, np.frexp(amax)[1] - 1 + 127, 0) - down, 1)
    scale = np.exp2(byte - 127.0)
    codes = (blocks / scale).astype(np.float32).astype(dtype).astype(np.float64)
    return np.moveaxis((codes * scale).reshape(v.shape), -1, axis)


WIDE = False


def mx_kscale(k):
    if not WIDE:
        return np.ones(k)
    levels = np.array([10, -10, 5, -5, 0])
    if k % 512:
        return np.exp2(np.random.permutation(np.resize(levels, k // 32))).repeat(32)
    a = np.empty((k // 512, 16))
    for p in range(k // 512):
        a[p, :8] = np.random.permutation(np.resize(levels, 8))
        for g in range(8):
            far = levels[np.abs(levels - a[p, g]) >= 10]
            a[p, g + 8] = far[np.random.randint(len(far))]
    return np.exp2(a.ravel()).repeat(32)


BF16 = ml_dtypes.bfloat16


def bf(x):
    return np.asarray(x, np.float32).astype(BF16)


def f64(x):
    return np.asarray(x).astype(np.float64)


B, S, D, H, QB = 1, 1024, 1024, 8, 512
HD = D // H
HALF = HD // 2


def rope_cache():
    inv_freq = 1.0 / (10000.0 ** (np.arange(HALF) / max(HALF, 1)))
    ang = np.arange(S)[:, None] * inv_freq[None, :]
    return np.cos(ang)[None, None], np.sin(ang)[None, None]


def apply_rope(u, cos, sin):
    u1, u2 = u[..., :HALF], u[..., HALF:]
    return np.concatenate([u1 * cos - u2 * sin, u1 * sin + u2 * cos], axis=-1)


def draw0():
    s = mx_kscale(D)
    return {"x": bf(np.random.standard_normal((B, S, D)) * s),
            "Wq": bf(np.random.standard_normal((2 * D, D)) / np.sqrt(D) / s[None, :]),
            "bq": bf(np.random.standard_normal(2 * D) * 0.2),
            "Wk": bf(np.random.standard_normal((2 * D, D)) / np.sqrt(D) / s[None, :]),
            "bk": bf(np.random.standard_normal(2 * D) * 0.2)}


def core(x, Wq, bq, Wk, bk):
    xq = mxq(f64(x), 2, "e4m3")
    q = ((xq @ mxq(f64(Wq), 1, "e4m3").T) + f64(bq)).reshape(B, S, H, 2 * HD).transpose(0, 2, 1, 3)
    k = ((xq @ mxq(f64(Wk), 1, "e4m3").T) + f64(bk)).reshape(B, S, H, 2 * HD).transpose(0, 2, 1, 3)
    cos, sin = rope_cache()
    q1, q2 = apply_rope(q[..., :HD], cos, sin), apply_rope(q[..., HD:], cos, sin)
    k1, k2 = apply_rope(k[..., :HD], cos, sin), apply_rope(k[..., HD:], cos, sin)
    return q1, q2, k1, k2


def e4m3fn_bytes(y):
    return np.clip(np.asarray(y, np.float64), -448.0, 448.0).astype(np.float32).astype(ml_dtypes.float8_e4m3fn).view(np.uint8)


def e4m3fn_values(b):
    return np.asarray(b, np.uint8).view(ml_dtypes.float8_e4m3fn).astype(np.float64)


def setup_inputs():
    d = draw0()
    x0 = np.asarray(d['Wq']).astype(np.float64)
    s = (np.max(np.abs(x0), axis=(0,), keepdims=True) / 448.0).astype(np.float32)
    out = {}
    for k, v in d.items():
        if k == 'Wq':
            out['Wq_bytes'] = e4m3fn_bytes(x0 / s.astype(np.float64))
            out['Wq_scale'] = s
        else:
            out[k] = v
    return out


def reference(x, Wq_bytes, Wq_scale, bq, Wk, bk):
    return core(x, e4m3fn_values(Wq_bytes) * Wq_scale.astype(np.float64), bq, Wk, bk)

@@ -1,0 +1,244 @@
+from contextlib import ExitStack
+import math
+
+import concourse.mybir as mybir
+from concourse.masks import make_identity
+
+FLOPS = 2 * 1024 * 1024 * 4096
+
+F32 = mybir.dt.float32
+BF16 = mybir.dt.bfloat16
+I32 = mybir.dt.int32
+U32 = mybir.dt.uint32
+U8 = mybir.dt.uint8
+FP8 = mybir.dt.float8_e4m3fn
+FP8X4 = mybir.dt.float8_e4m3fn_x4
+ALU = mybir.AluOpType
+ACT = mybir.ActivationFunctionType
+
+P = 128
+D = 1024
+HALF = 64
+TWO_PI = 2.0 * math.pi
+PI_HI = 6.28125
+PI_LO = TWO_PI - PI_HI
+
+
+def tile_differentialselfattention_pa_kernel(
+    tc, x, Wq_bytes, Wq_scale, bq, Wk, bk, out_0, out_1, out_2, out_3
+):
+    nc = tc.nc
+    with ExitStack() as ctx:
+        const = ctx.enter_context(tc.tile_pool(name="const", bufs=1))
+        wbf_pool = ctx.enter_context(tc.tile_pool(name="wbf", bufs=3))
+        grp_pool = ctx.enter_context(tc.tile_pool(name="grp", bufs=2))
+        code_pool = ctx.enter_context(tc.tile_pool(name="code", bufs=3))
+        psum_in = ctx.enter_context(tc.psum_pool(name="psum_in", bufs=2))
+        psum_mx = ctx.enter_context(tc.psum_pool(name="psum_mx", bufs=3))
+        psum_bk = ctx.enter_context(tc.psum_pool(name="psum_bk", bufs=3))
+
+        wq_view = Wq_bytes.rearrange("(c p) k -> p c k", p=P)
+        wk_view = Wk.rearrange("(c p) k -> p c k", p=P)
+        x_view = x.rearrange("b (p a) k -> p (b a) k", a=8)
+        out_views = [o.rearrange("b h (p a) f -> p (b h) a f", a=8) for o in (out_0, out_1, out_2, out_3)]
+
+        sc_bc = const.tile([P, D], F32, name="sc_bc")
+        wq_bytes = [const.tile([P, 4, D], U8, name="wq_bytes%d" % c) for c in range(4)]
+        wk_rows = [const.tile([P, 4, D], BF16, name="wk_rows%d" % c) for c in range(4)]
+        x_half = [const.tile([P, 4, D], BF16, name="x_half%d" % h) for h in range(2)]
+        brow = const.tile([P, P], BF16, name="brow")
+        nc.gpsimd.memset(brow[:], 0.0)
+
+        def load_wk(c):
+            nc.sync.dma_start(out=wk_rows[c][:], in_=wk_view[:, 4 * c:4 * c + 4, :])
+
+        def load_wq(c):
+            nc.sync.dma_start(out=wq_bytes[c][:], in_=wq_view[:, 4 * c:4 * c + 4, :])
+
+        nc.sync.dma_start(out=x_half[0][:], in_=x_view[:, 0:4, :])
+        load_wk(0)
+        nc.sync.dma_start(out=brow[0:16, :], in_=bq.rearrange("(r c) -> r c", c=P))
+        nc.sync.dma_start(out=brow[16:32, :], in_=bk.rearrange("(r c) -> r c", c=P))
+        nc.sync.dma_start(out=x_half[1][:], in_=x_view[:, 4:8, :])
+        load_wk(1)
+        nc.sync.dma_start(out=sc_bc[:], in_=Wq_scale.rearrange("o k -> (o k)").partition_broadcast(P))
+        load_wq(0)
+        load_wk(2)
+        load_wq(1)
+        load_wk(3)
+        load_wq(2)
+        load_wq(3)
+
+        zero1 = const.tile([P, 1], F32, name="zero1")
+        nc.vector.memset(zero1[:], 0.0)
+        warm = const.tile([P, 1], F32, name="warm")
+        nc.scalar.activation(out=warm[:], in_=zero1[:], func=ACT.Sin)
+
+        tab = const.tile([P, 8, 2, P], F32, name="tab")
+        ident_f = const.tile([P, P], F32, name="ident_f")
+        ident_b = const.tile([P, P], BF16, name="ident_b")
+        with tc.tile_pool(name="trig", bufs=1) as trig:
+            tok_f = trig.tile([P, 8], F32, name="tok_f")
+            nc.gpsimd.iota(
+                tok_f[:], pattern=[[1, 8]], base=0, channel_multiplier=8, allow_small_or_imprecise_dtypes=True
+            )
+            ones8 = trig.tile([P, 8], F32, name="ones8")
+            nc.gpsimd.memset(ones8[:], 1.0)
+            make_identity(nc, ident_f[:])
+            freq_hi = trig.tile([P, 8, 8], F32, name="freq_hi")
+            freq = trig.tile([P, 8, 8], F32, name="freq")
+            for j in range(8):
+                nc.gpsimd.tensor_scalar(
+                    out=freq_hi[:, j, :], in0=ones8[:], scalar1=10000.0 ** (-8.0 * j / HALF), scalar2=0.0,
+                    op0=ALU.mult, op1=ALU.add,
+                )
+            for j in range(8):
+                nc.gpsimd.tensor_scalar(
+                    out=freq[:, :, j], in0=freq_hi[:, :, j], scalar1=10000.0 ** (-1.0 * j / HALF), scalar2=0.0,
+                    op0=ALU.mult, op1=ALU.add,
+                )
+            make_identity(nc, ident_b[:])
+            theta = trig.tile([P, 8, HALF], F32, name="theta")
+            nc.vector.tensor_tensor(
+                out=theta[:],
+                in0=tok_f[:].unsqueeze(2).to_broadcast([P, 8, HALF]),
+                in1=freq[:].rearrange("p a b -> p (a b)").unsqueeze(1).to_broadcast([P, 8, HALF]),
+                op=ALU.mult,
+            )
+            th2 = theta[:].rearrange("p a i -> p (a i)")
+            turns_i = trig.tile([P, 8 * HALF], I32, name="turns_i")
+            nc.vector.tensor_scalar(out=turns_i[:], in0=th2, scalar1=1.0 / TWO_PI, scalar2=None, op0=ALU.mult)
+            turns = trig.tile([P, 8 * HALF], F32, name="turns")
+            nc.vector.tensor_copy(out=turns[:], in_=turns_i[:])
+            ang_s = trig.tile([P, 8, HALF], F32, name="ang_s")
+            as2 = ang_s[:].rearrange("p a i -> p (a i)")
+            nc.vector.scalar_tensor_tensor(out=as2, in0=turns[:], scalar=-PI_HI, in1=th2, op0=ALU.mult, op1=ALU.add)
+            nc.vector.scalar_tensor_tensor(out=as2, in0=turns[:], scalar=-PI_LO, in1=as2, op0=ALU.mult, op1=ALU.add)
+            mask = trig.tile([P, 8 * HALF], F32, name="mask")
+            nc.vector.tensor_scalar(out=mask[:], in0=as2, scalar1=math.pi, scalar2=None, op0=ALU.is_gt)
+            nc.vector.scalar_tensor_tensor(out=as2, in0=mask[:], scalar=-TWO_PI, in1=as2, op0=ALU.mult, op1=ALU.add)
+            mask2 = trig.tile([P, 8 * HALF], F32, name="mask2")
+            nc.vector.tensor_scalar(out=mask2[:], in0=as2, scalar1=-math.pi, scalar2=None, op0=ALU.is_lt)
+            nc.vector.scalar_tensor_tensor(out=as2, in0=mask2[:], scalar=TWO_PI, in1=as2, op0=ALU.mult, op1=ALU.add)
+            ang_c = trig.tile([P, 8, HALF], F32, name="ang_c")
+            ac2 = ang_c[:].rearrange("p a i -> p (a i)")
+            nc.vector.scalar_tensor_tensor(out=ac2, in0=as2, scalar=-1.0, in1=as2, op0=ALU.mult, op1=ALU.min)
+            nc.vector.tensor_scalar(out=ac2, in0=ac2, scalar1=0.5 * math.pi, scalar2=None, op0=ALU.add)
+            nc.scalar.activation(out=tab[:, :, 0, 0:HALF], in_=ang_c[:], func=ACT.Sin)
+            nc.scalar.activation(out=tab[:, :, 0, HALF:P], in_=ang_s[:], func=ACT.Sin, scale=-1.0)
+            nc.scalar.activation(out=tab[:, :, 1, 0:HALF], in_=ang_s[:], func=ACT.Sin)
+            nc.scalar.activation(out=tab[:, :, 1, HALF:P], in_=ang_c[:], func=ACT.Sin)
+
+        tb_pool = ctx.enter_context(tc.tile_pool(name="tb", bufs=8))
+        prod_pool = ctx.enter_context(tc.tile_pool(name="prod", bufs=5))
+        rot_pool = ctx.enter_context(tc.tile_pool(name="rot", bufs=3))
+
+        pb = psum_in.tile([P, P], BF16, tag="pin")
+        nc.tensor.transpose(pb[:], brow[:], ident_b[:])
+        bias_f = const.tile([P, 32], F32, name="bias_f")
+        nc.vector.tensor_copy(out=bias_f[:], in_=pb[:, 0:32])
+
+        def widen(c):
+            wide = wbf_pool.tile([P, 4, D], BF16, tag="wbf")
+            for s in range(4):
+                nc.vector.tensor_tensor(
+                    out=wide[:, s, :], in0=wq_bytes[c][:, s, :].bitcast(FP8), in1=sc_bc[:], op=ALU.mult
+                )
+            return wide
+
+        def prepare(rows, codes, scales):
+            grouped = grp_pool.tile([P, 2, 512, 4], BF16, tag="grouped", align_bytes=64)
+            for s in range(4):
+                words = rows[:, s, :].bitcast(F32)
+                pin = psum_in.tile([P, 2, 2, P], F32, tag="pin")
+                for g in range(2):
+                    for u in range(2):
+                        nc.tensor.transpose(pin[:, g, u, :], words[:, 256 * g + u:256 * (g + 1):2], ident_f[:])
+                nc.scalar.copy(
+                    out=grouped[:, :, P * s:P * (s + 1), :].bitcast(F32),
+                    in_=pin[:].rearrange("p g u r -> p g r u"),
+                )
+            nc.vector.quantize_mx(
+                out=codes[:].rearrange("p g c -> p (g c)").bitcast(FP8X4),
+                scales=scales[:].rearrange("p g c -> p (g c)"),
+                in_=grouped[:].rearrange("p g r t -> p (g r t)"),
+            )
+
+        def prepare_w(rows):
+            codes = code_pool.tile([P, 2, 512], U32, tag="wcodes", align_bytes=64)
+            scales = code_pool.tile([P, 2, 512], U8, tag="wscales", align_bytes=64)
+            prepare(rows, codes, scales)
+            return codes, scales
+
+        x_codes = [const.tile([P, 2, 512], U32, name="x_codes%d" % h, align_bytes=64) for h in range(2)]
+        x_scales = [const.tile([P, 2, 512], U8, name="x_scales%d" % h, align_bytes=64) for h in range(2)]
+
+        def project(c, h, wcs):
+            codes, scales = wcs
+            res = []
+            for s in range(4):
+                acc = psum_mx.tile([P, 512], F32, tag="acc")
+                for g in range(2):
+                    nc.tensor.matmul_mx(
+                        out=acc[:],
+                        lhsT=codes[:, g, P * s:P * (s + 1)].bitcast(FP8X4),
+                        lhsT_scale=scales[:, g, P * s:P * (s + 1)],
+                        rhs=x_codes[h][:, g, :].bitcast(FP8X4),
+                        rhs_scale=x_scales[h][:, g, :],
+                        start=(g == 0),
+                        stop=(g == 1),
+                    )
+                tb = tb_pool.tile([P, 512], F32, tag="tb")
+                nc.scalar.activation(
+                    out=tb[:], in_=acc[:], func=ACT.Identity, bias=bias_f[:, 4 * c + s:4 * c + s + 1], scale=1.0
+                )
+                res.append(tb)
+            return res
+
+        def rotate(c, h, tbs):
+            rot = rot_pool.tile([P, 4, 4, P], F32, tag="rot")
+            for al in range(4):
+                back = psum_bk.tile([P, 4, P], F32, tag="back")
+                for s in range(4):
+                    nc.tensor.transpose(back[:, s, :], tbs[s][:, P * al:P * (al + 1)], ident_f[:])
+                prod = prod_pool.tile([P, 4, 2, P], F32, tag="prod")
+                nc.vector.tensor_tensor(
+                    out=prod[:],
+                    in0=back[:].unsqueeze(2).to_broadcast([P, 4, 2, P]),
+                    in1=tab[:, 4 * h + al].unsqueeze(1).to_broadcast([P, 4, 2, P]),
+                    op=ALU.mult,
+                )
+                nc.gpsimd.tensor_tensor(
+                    out=rot[:, :, al, :].rearrange("p s (o i) -> p s o i", o=2),
+                    in0=prod[:, :, :, 0:HALF],
+                    in1=prod[:, :, :, HALF:P],
+                    op=ALU.add,
+                )
+            for sub in range(2):
+                head = 2 * (c % 4)
+                nc.sync.dma_start(
+                    out=out_views[2 * (c // 4) + sub][:, head:head + 2, 4 * h:4 * h + 4, :],
+                    in_=rot[:, sub::2, :, :],
+                )
+
+        order = [4, 5, 0, 6, 1, 7, 2, 3]
+
+        def ready(c):
+            return prepare_w(widen(c) if c < 4 else wk_rows[c - 4])
+
+        wcs = {}
+        prepare(x_half[0], x_codes[0], x_scales[0])
+        wcs[order[0]] = ready(order[0])
+        cur = project(order[0], 0, wcs[order[0]])
+        prepare(x_half[1], x_codes[1], x_scales[1])
+        wcs[order[1]] = ready(order[1])
+        for unit in range(16):
+            pos, h = divmod(unit, 2)
+            nxt = None
+            if unit + 1 < 16:
+                pos2, h2 = divmod(unit + 1, 2)
+                nxt = project(order[pos2], h2, wcs[order[pos2]])
+            if h == 0 and pos + 2 < 8:
+                wcs[order[pos + 2]] = ready(order[pos + 2])
+            rotate(order[pos], h, cur)
+            cur = nxt

@@ -30,12 +30,15 @@ def tile_differentialselfattention_pa_kernel(
     nc = tc.nc
     with ExitStack() as ctx:
         const = ctx.enter_context(tc.tile_pool(name="const", bufs=1))
+        cast_pool = ctx.enter_context(tc.tile_pool(name="cast", bufs=2))
         wbf_pool = ctx.enter_context(tc.tile_pool(name="wbf", bufs=3))
         grp_pool = ctx.enter_context(tc.tile_pool(name="grp", bufs=2))
         code_pool = ctx.enter_context(tc.tile_pool(name="code", bufs=3))
-        psum_in = ctx.enter_context(tc.psum_pool(name="psum_in", bufs=2))
-        psum_mx = ctx.enter_context(tc.psum_pool(name="psum_mx", bufs=3))
-        psum_bk = ctx.enter_context(tc.psum_pool(name="psum_bk", bufs=3))
+        term_pool = ctx.enter_context(tc.tile_pool(name="term", bufs=8))
+        rot_pool = ctx.enter_context(tc.tile_pool(name="rot", bufs=3))
+        psum_tp = ctx.enter_context(tc.psum_pool(name="psum_tp", bufs=4))
+        psum_mx = ctx.enter_context(tc.psum_pool(name="psum_mx", bufs=4))
+        ctx.enter_context(tc.manual_schedule())
 
         wq_view = Wq_bytes.rearrange("(c p) k -> p c k", p=P)
         wk_view = Wk.rearrange("(c p) k -> p c k", p=P)
@@ -49,133 +52,140 @@ def tile_differentialselfattention_pa_kernel(
         brow = const.tile([P, P], BF16, name="brow")
         nc.gpsimd.memset(brow[:], 0.0)
 
-        def load_wk(c):
-            nc.sync.dma_start(out=wk_rows[c][:], in_=wk_view[:, 4 * c:4 * c + 4, :])
+        def load_rows(tile, view, first, pieces):
+            step = 4 // pieces
+            for j in range(pieces):
+                nc.sync.dma_start(
+                    out=tile[:, step * j:step * (j + 1), :], in_=view[:, first + step * j:first + step * (j + 1), :]
+                )
 
-        def load_wq(c):
-            nc.sync.dma_start(out=wq_bytes[c][:], in_=wq_view[:, 4 * c:4 * c + 4, :])
-
-        nc.sync.dma_start(out=x_half[0][:], in_=x_view[:, 0:4, :])
-        load_wk(0)
+        load_rows(x_half[0], x_view, 0, 4)
+        load_rows(wk_rows[0], wk_view, 0, 4)
         nc.sync.dma_start(out=brow[0:16, :], in_=bq.rearrange("(r c) -> r c", c=P))
         nc.sync.dma_start(out=brow[16:32, :], in_=bk.rearrange("(r c) -> r c", c=P))
-        nc.sync.dma_start(out=x_half[1][:], in_=x_view[:, 4:8, :])
-        load_wk(1)
+        load_rows(x_half[1], x_view, 4, 2)
+        load_rows(wk_rows[1], wk_view, 4, 2)
         nc.sync.dma_start(out=sc_bc[:], in_=Wq_scale.rearrange("o k -> (o k)").partition_broadcast(P))
-        load_wq(0)
-        load_wk(2)
-        load_wq(1)
-        load_wk(3)
-        load_wq(2)
-        load_wq(3)
+        load_rows(wq_bytes[0], wq_view, 0, 1)
+        load_rows(wk_rows[2], wk_view, 8, 1)
+        load_rows(wq_bytes[1], wq_view, 4, 1)
+        load_rows(wk_rows[3], wk_view, 12, 1)
+        load_rows(wq_bytes[2], wq_view, 8, 1)
+        load_rows(wq_bytes[3], wq_view, 12, 1)
 
         zero1 = const.tile([P, 1], F32, name="zero1")
         nc.vector.memset(zero1[:], 0.0)
         warm = const.tile([P, 1], F32, name="warm")
         nc.scalar.activation(out=warm[:], in_=zero1[:], func=ACT.Sin)
 
-        tab = const.tile([P, 8, 2, P], F32, name="tab")
         ident_f = const.tile([P, P], F32, name="ident_f")
+        swap_f = const.tile([P, P], F32, name="swap_f")
         ident_b = const.tile([P, P], BF16, name="ident_b")
-        with tc.tile_pool(name="trig", bufs=1) as trig:
-            tok_f = trig.tile([P, 8], F32, name="tok_f")
-            nc.gpsimd.iota(
-                tok_f[:], pattern=[[1, 8]], base=0, channel_multiplier=8, allow_small_or_imprecise_dtypes=True
-            )
-            ones8 = trig.tile([P, 8], F32, name="ones8")
-            nc.gpsimd.memset(ones8[:], 1.0)
-            make_identity(nc, ident_f[:])
-            freq_hi = trig.tile([P, 8, 8], F32, name="freq_hi")
-            freq = trig.tile([P, 8, 8], F32, name="freq")
-            for j in range(8):
-                nc.gpsimd.tensor_scalar(
-                    out=freq_hi[:, j, :], in0=ones8[:], scalar1=10000.0 ** (-8.0 * j / HALF), scalar2=0.0,
-                    op0=ALU.mult, op1=ALU.add,
-                )
-            for j in range(8):
-                nc.gpsimd.tensor_scalar(
-                    out=freq[:, :, j], in0=freq_hi[:, :, j], scalar1=10000.0 ** (-1.0 * j / HALF), scalar2=0.0,
-                    op0=ALU.mult, op1=ALU.add,
-                )
-            make_identity(nc, ident_b[:])
-            theta = trig.tile([P, 8, HALF], F32, name="theta")
-            nc.vector.tensor_tensor(
-                out=theta[:],
-                in0=tok_f[:].unsqueeze(2).to_broadcast([P, 8, HALF]),
-                in1=freq[:].rearrange("p a b -> p (a b)").unsqueeze(1).to_broadcast([P, 8, HALF]),
-                op=ALU.mult,
-            )
-            th2 = theta[:].rearrange("p a i -> p (a i)")
-            turns_i = trig.tile([P, 8 * HALF], I32, name="turns_i")
-            nc.vector.tensor_scalar(out=turns_i[:], in0=th2, scalar1=1.0 / TWO_PI, scalar2=None, op0=ALU.mult)
-            turns = trig.tile([P, 8 * HALF], F32, name="turns")
-            nc.vector.tensor_copy(out=turns[:], in_=turns_i[:])
-            ang_s = trig.tile([P, 8, HALF], F32, name="ang_s")
-            as2 = ang_s[:].rearrange("p a i -> p (a i)")
-            nc.vector.scalar_tensor_tensor(out=as2, in0=turns[:], scalar=-PI_HI, in1=th2, op0=ALU.mult, op1=ALU.add)
-            nc.vector.scalar_tensor_tensor(out=as2, in0=turns[:], scalar=-PI_LO, in1=as2, op0=ALU.mult, op1=ALU.add)
-            mask = trig.tile([P, 8 * HALF], F32, name="mask")
-            nc.vector.tensor_scalar(out=mask[:], in0=as2, scalar1=math.pi, scalar2=None, op0=ALU.is_gt)
-            nc.vector.scalar_tensor_tensor(out=as2, in0=mask[:], scalar=-TWO_PI, in1=as2, op0=ALU.mult, op1=ALU.add)
-            mask2 = trig.tile([P, 8 * HALF], F32, name="mask2")
-            nc.vector.tensor_scalar(out=mask2[:], in0=as2, scalar1=-math.pi, scalar2=None, op0=ALU.is_lt)
-            nc.vector.scalar_tensor_tensor(out=as2, in0=mask2[:], scalar=TWO_PI, in1=as2, op0=ALU.mult, op1=ALU.add)
-            ang_c = trig.tile([P, 8, HALF], F32, name="ang_c")
-            ac2 = ang_c[:].rearrange("p a i -> p (a i)")
-            nc.vector.scalar_tensor_tensor(out=ac2, in0=as2, scalar=-1.0, in1=as2, op0=ALU.mult, op1=ALU.min)
-            nc.vector.tensor_scalar(out=ac2, in0=ac2, scalar1=0.5 * math.pi, scalar2=None, op0=ALU.add)
-            nc.scalar.activation(out=tab[:, :, 0, 0:HALF], in_=ang_c[:], func=ACT.Sin)
-            nc.scalar.activation(out=tab[:, :, 0, HALF:P], in_=ang_s[:], func=ACT.Sin, scale=-1.0)
-            nc.scalar.activation(out=tab[:, :, 1, 0:HALF], in_=ang_s[:], func=ACT.Sin)
-            nc.scalar.activation(out=tab[:, :, 1, HALF:P], in_=ang_c[:], func=ACT.Sin)
+        tok_f = const.tile([P, 8], F32, name="tok_f")
+        make_identity(nc, ident_f[:])
+        nc.gpsimd.iota(tok_f[:], pattern=[[1, 8]], base=0, channel_multiplier=8, allow_small_or_imprecise_dtypes=True)
+        nc.gpsimd.tensor_copy(out=swap_f[:, 0:HALF], in_=ident_f[:, HALF:P])
+        nc.gpsimd.tensor_copy(out=swap_f[:, HALF:P], in_=ident_f[:, 0:HALF])
+        make_identity(nc, ident_b[:])
 
-        tb_pool = ctx.enter_context(tc.tile_pool(name="tb", bufs=8))
-        prod_pool = ctx.enter_context(tc.tile_pool(name="prod", bufs=5))
-        rot_pool = ctx.enter_context(tc.tile_pool(name="rot", bufs=3))
+        freq = const.tile([P, HALF], F32, name="freq")
+        nc.vector.memset(freq[:, 0:1], 1.0)
+        for w in (1, 2, 4, 8, 16, 32):
+            nc.vector.tensor_scalar(
+                out=freq[:, w:2 * w], in0=freq[:, 0:w], scalar1=10000.0 ** (-1.0 * w / HALF), scalar2=None, op0=ALU.mult
+            )
+        theta = const.tile([P, 8, HALF], F32, name="theta")
+        nc.vector.tensor_tensor(
+            out=theta[:],
+            in0=tok_f[:].unsqueeze(2).to_broadcast([P, 8, HALF]),
+            in1=freq[:].unsqueeze(1).to_broadcast([P, 8, HALF]),
+            op=ALU.mult,
+        )
+        th2 = theta[:].rearrange("p a i -> p (a i)")
+        turns_i = const.tile([P, 8 * HALF], I32, name="turns_i")
+        nc.vector.tensor_scalar(out=turns_i[:], in0=th2, scalar1=1.0 / TWO_PI, scalar2=None, op0=ALU.mult)
+        turns = const.tile([P, 8 * HALF], F32, name="turns")
+        nc.vector.tensor_copy(out=turns[:], in_=turns_i[:])
+        ang_s = const.tile([P, 8, HALF], F32, name="ang_s")
+        as2 = ang_s[:].rearrange("p a i -> p (a i)")
+        nc.vector.scalar_tensor_tensor(out=as2, in0=turns[:], scalar=-PI_HI, in1=th2, op0=ALU.mult, op1=ALU.add)
+        nc.vector.scalar_tensor_tensor(out=as2, in0=turns[:], scalar=-PI_LO, in1=as2, op0=ALU.mult, op1=ALU.add)
+        ang_c = const.tile([P, 8, HALF], F32, name="ang_c")
+        ac2 = ang_c[:].rearrange("p a i -> p (a i)")
+        nc.vector.scalar_tensor_tensor(out=ac2, in0=as2, scalar=-1.0, in1=as2, op0=ALU.mult, op1=ALU.min)
+        nc.vector.tensor_scalar(out=ac2, in0=ac2, scalar1=0.5 * math.pi, scalar2=None, op0=ALU.add)
 
-        pb = psum_in.tile([P, P], BF16, tag="pin")
-        nc.tensor.transpose(pb[:], brow[:], ident_b[:])
+        tab_rows = const.tile([P, 8, 2, P], F32, name="tab_rows")
+        tab_cols = const.tile([P, 2, 2, 512], F32, name="tab_cols")
         bias_f = const.tile([P, 32], F32, name="bias_f")
-        nc.vector.tensor_copy(out=bias_f[:], in_=pb[:, 0:32])
 
-        def widen(c):
-            wide = wbf_pool.tile([P, 4, D], BF16, tag="wbf")
-            for s in range(4):
-                nc.vector.tensor_tensor(
-                    out=wide[:, s, :], in0=wq_bytes[c][:, s, :].bitcast(FP8), in1=sc_bc[:], op=ALU.mult
-                )
-            return wide
+        def sines():
+            nc.scalar.activation(out=tab_rows[:, :, 0, 0:HALF], in_=ang_c[:], func=ACT.Sin)
+            nc.scalar.activation(out=tab_rows[:, :, 0, HALF:P], in_=ang_c[:], func=ACT.Sin)
+            nc.scalar.activation(out=tab_rows[:, :, 1, 0:HALF], in_=ang_s[:], func=ACT.Sin)
+            nc.scalar.activation(out=tab_rows[:, :, 1, HALF:P], in_=ang_s[:], func=ACT.Sin, scale=-1.0)
 
-        def prepare(rows, codes, scales):
+        def out_of_psum(on_vector, out, in_):
+            if on_vector:
+                nc.vector.tensor_copy(out=out, in_=in_)
+            else:
+                nc.scalar.copy(out=out, in_=in_)
+
+        def turn_table(h, o, on_vector):
+            bank = psum_tp.tile([P, 4, P], F32, tag="tp")
+            for al in range(4):
+                nc.tensor.transpose(bank[:, al, :], tab_rows[:, 4 * h + al, o, :], ident_f[:])
+            out_of_psum(on_vector, tab_cols[:, o, h, :], bank[:].rearrange("p a r -> p (a r)"))
+
+        def turn_bias():
+            pb = psum_tp.tile([P, P], BF16, tag="tp")
+            nc.tensor.transpose(pb[:], brow[:], ident_b[:])
+            nc.vector.tensor_copy(out=bias_f[:], in_=pb[:, 0:32])
+
+        def turn_rows(rows, s, grouped, on_vector):
+            words = rows[:, s, :].bitcast(F32)
+            pin = psum_tp.tile([P, 2, 2, P], F32, tag="tp")
+            for g in range(2):
+                for u in range(2):
+                    nc.tensor.transpose(pin[:, g, u, :], words[:, 256 * g + u:256 * (g + 1):2], ident_f[:])
+            out_of_psum(
+                on_vector, grouped[:, :, P * s:P * (s + 1), :].bitcast(F32), pin[:].rearrange("p g u r -> p g r u")
+            )
+
+        def new_grouped():
             grouped = grp_pool.tile([P, 2, 512, 4], BF16, tag="grouped", align_bytes=64)
-            for s in range(4):
-                words = rows[:, s, :].bitcast(F32)
-                pin = psum_in.tile([P, 2, 2, P], F32, tag="pin")
-                for g in range(2):
-                    for u in range(2):
-                        nc.tensor.transpose(pin[:, g, u, :], words[:, 256 * g + u:256 * (g + 1):2], ident_f[:])
-                nc.scalar.copy(
-                    out=grouped[:, :, P * s:P * (s + 1), :].bitcast(F32),
-                    in_=pin[:].rearrange("p g u r -> p g r u"),
-                )
+            return grouped
+
+        def quantise(grouped, codes, scales):
             nc.vector.quantize_mx(
                 out=codes[:].rearrange("p g c -> p (g c)").bitcast(FP8X4),
                 scales=scales[:].rearrange("p g c -> p (g c)"),
                 in_=grouped[:].rearrange("p g r t -> p (g r t)"),
             )
 
-        def prepare_w(rows):
+        def new_codes():
             codes = code_pool.tile([P, 2, 512], U32, tag="wcodes", align_bytes=64)
             scales = code_pool.tile([P, 2, 512], U8, tag="wscales", align_bytes=64)
-            prepare(rows, codes, scales)
             return codes, scales
 
         x_codes = [const.tile([P, 2, 512], U32, name="x_codes%d" % h, align_bytes=64) for h in range(2)]
         x_scales = [const.tile([P, 2, 512], U8, name="x_scales%d" % h, align_bytes=64) for h in range(2)]
 
+        def widen(wide, c, s, on_vector):
+            if on_vector:
+                nc.vector.tensor_tensor(
+                    out=wide[:, s, :], in0=wq_bytes[c][:, s, :].bitcast(FP8), in1=sc_bc[:], op=ALU.mult
+                )
+            else:
+                cast = cast_pool.tile([P, D], BF16, tag="cast")
+                nc.scalar.copy(out=cast[:], in_=wq_bytes[c][:, s, :].bitcast(FP8))
+                for j in range(2):
+                    cols = slice(512 * j, 512 * (j + 1))
+                    nc.gpsimd.tensor_tensor(out=wide[:, s, cols], in0=cast[:, cols], in1=sc_bc[:, cols], op=ALU.mult)
+
         def project(c, h, wcs):
             codes, scales = wcs
-            res = []
+            accs = []
             for s in range(4):
                 acc = psum_mx.tile([P, 512], F32, tag="acc")
                 for g in range(2):
@@ -188,57 +198,121 @@ def tile_differentialselfattention_pa_kernel(
                         start=(g == 0),
                         stop=(g == 1),
                     )
-                tb = tb_pool.tile([P, 512], F32, tag="tb")
-                nc.scalar.activation(
-                    out=tb[:], in_=acc[:], func=ACT.Identity, bias=bias_f[:, 4 * c + s:4 * c + s + 1], scale=1.0
-                )
-                res.append(tb)
-            return res
+                accs.append(acc)
+            return accs
 
-        def rotate(c, h, tbs):
-            rot = rot_pool.tile([P, 4, 4, P], F32, tag="rot")
+        def products(c, h, accs):
+            terms = []
+            for s in range(4):
+                term = term_pool.tile([P, 2, 512], F32, tag="term")
+                nc.vector.scalar_tensor_tensor(
+                    out=term[:],
+                    in0=accs[s][:].unsqueeze(1).to_broadcast([P, 2, 512]),
+                    scalar=bias_f[:, 4 * c + s:4 * c + s + 1],
+                    in1=tab_cols[:, :, h, :],
+                    op0=ALU.add,
+                    op1=ALU.mult,
+                )
+                terms.append(term)
+            return terms
+
+        def turn_back(term, rot, s):
+            bank = psum_tp.tile([P, 4, P], F32, tag="tp")
             for al in range(4):
-                back = psum_bk.tile([P, 4, P], F32, tag="back")
-                for s in range(4):
-                    nc.tensor.transpose(back[:, s, :], tbs[s][:, P * al:P * (al + 1)], ident_f[:])
-                prod = prod_pool.tile([P, 4, 2, P], F32, tag="prod")
-                nc.vector.tensor_tensor(
-                    out=prod[:],
-                    in0=back[:].unsqueeze(2).to_broadcast([P, 4, 2, P]),
-                    in1=tab[:, 4 * h + al].unsqueeze(1).to_broadcast([P, 4, 2, P]),
-                    op=ALU.mult,
+                cols = slice(P * al, P * (al + 1))
+                nc.tensor.matmul(
+                    out=bank[:, al, :], lhsT=term[:, 0, cols], rhs=ident_f[:], is_transpose=True, start=True, stop=False
                 )
-                nc.gpsimd.tensor_tensor(
-                    out=rot[:, :, al, :].rearrange("p s (o i) -> p s o i", o=2),
-                    in0=prod[:, :, :, 0:HALF],
-                    in1=prod[:, :, :, HALF:P],
-                    op=ALU.add,
+                nc.tensor.matmul(
+                    out=bank[:, al, :], lhsT=term[:, 1, cols], rhs=swap_f[:], is_transpose=True, start=False, stop=True
                 )
-            for sub in range(2):
-                head = 2 * (c % 4)
+            nc.scalar.copy(out=rot[:, s, :, :], in_=bank[:])
+
+        def store(c, h, rot, subs):
+            head = 2 * (c % 4)
+            for sub in subs:
                 nc.sync.dma_start(
-                    out=out_views[2 * (c // 4) + sub][:, head:head + 2, 4 * h:4 * h + 4, :],
-                    in_=rot[:, sub::2, :, :],
+                    out=out_views[2 * (c // 4) + sub][:, head:head + 2, 4 * h:4 * h + 4, :], in_=rot[:, sub::2, :, :]
                 )
 
-        order = [4, 5, 0, 6, 1, 7, 2, 3]
-
-        def ready(c):
-            return prepare_w(widen(c) if c < 4 else wk_rows[c - 4])
-
+        order = [4, 5, 6, 7, 0, 1, 2, 3]
+        units = [(c, h) for c in order for h in range(2)]
+        wides = {}
+        groupeds = {}
         wcs = {}
-        prepare(x_half[0], x_codes[0], x_scales[0])
-        wcs[order[0]] = ready(order[0])
-        cur = project(order[0], 0, wcs[order[0]])
-        prepare(x_half[1], x_codes[1], x_scales[1])
-        wcs[order[1]] = ready(order[1])
-        for unit in range(16):
-            pos, h = divmod(unit, 2)
+
+        def rows_of(c):
+            return wides[c] if c < 4 else wk_rows[c - 4]
+
+        gx0 = new_grouped()
+        for s in range(4):
+            turn_rows(x_half[0], s, gx0, False)
+        quantise(gx0, x_codes[0], x_scales[0])
+        g0 = new_grouped()
+        for s in range(4):
+            turn_rows(rows_of(order[0]), s, g0, s >= 2)
+        wcs[order[0]] = new_codes()
+        quantise(g0, wcs[order[0]][0], wcs[order[0]][1])
+        sines()
+        turn_bias()
+        gx1 = new_grouped()
+        for s in range(4):
+            turn_rows(x_half[1], s, gx1, s % 2 == 0)
+        quantise(gx1, x_codes[1], x_scales[1])
+        accs = project(units[0][0], units[0][1], wcs[units[0][0]])
+        for o in range(2):
+            turn_table(0, o, o == 0)
+        terms = products(units[0][0], units[0][1], accs)
+        for o in range(2):
+            turn_table(1, o, False)
+        g1 = new_grouped()
+        for s in range(4):
+            turn_rows(rows_of(order[1]), s, g1, False)
+        wcs[order[1]] = new_codes()
+        quantise(g1, wcs[order[1]][0], wcs[order[1]][1])
+
+        jobs = [(order[k], s) for k in range(2, 8) for s in range(4)]
+        widen_plan = {}
+        tile_no = 0
+        for b in range(11):
+            widen_plan[b] = []
+            for on_vector in ((False, True) if b % 2 == 0 and b < 10 else (False,)):
+                if tile_no < 16:
+                    widen_plan[b].append((tile_no // 4, tile_no % 4, on_vector))
+                    tile_no += 1
+
+        def prep_job(b, j):
+            if 2 * b + j >= len(jobs):
+                return
+            c, s = jobs[2 * b + j]
+            if s == 0:
+                groupeds[c] = new_grouped()
+            turn_rows(rows_of(c), s, groupeds[c], False)
+
+        for n in range(16):
+            c, h = units[n]
             nxt = None
-            if unit + 1 < 16:
-                pos2, h2 = divmod(unit + 1, 2)
-                nxt = project(order[pos2], h2, wcs[order[pos2]])
-            if h == 0 and pos + 2 < 8:
-                wcs[order[pos + 2]] = ready(order[pos + 2])
-            rotate(order[pos], h, cur)
-            cur = nxt
+            if n + 1 < 16:
+                c2, h2 = units[n + 1]
+                accs = project(c2, h2, wcs[c2])
+                nxt = products(c2, h2, accs)
+            rot = rot_pool.tile([P, 4, 4, P], F32, tag="rot")
+            turn_back(terms[0], rot, 0)
+            prep_job(n, 0)
+            turn_back(terms[1], rot, 1)
+            prep_job(n, 1)
+            for cq, s, on_vector in widen_plan.get(n, []):
+                if s == 0:
+                    wide = wbf_pool.tile([P, 4, D], BF16, tag="wbf")
+                    wides[cq] = wide
+                widen(wides[cq], cq, s, on_vector)
+            turn_back(terms[2], rot, 2)
+            if n == 15:
+                store(c, h, rot, [0])
+            turn_back(terms[3], rot, 3)
+            store(c, h, rot, [1] if n == 15 else [0, 1])
+            if 2 * n + 1 < len(jobs) and jobs[2 * n + 1][1] == 3:
+                cj = jobs[2 * n + 1][0]
+                wcs[cj] = new_codes()
+                quantise(groupeds[cj], wcs[cj][0], wcs[cj][1])
+            terms = nxt

@@ -30,7 +30,7 @@ def tile_differentialselfattention_pa_kernel(
     nc = tc.nc
     with ExitStack() as ctx:
         const = ctx.enter_context(tc.tile_pool(name="const", bufs=1))
-        cast_pool = ctx.enter_context(tc.tile_pool(name="cast", bufs=2))
+        cast_pool = ctx.enter_context(tc.tile_pool(name="cast", bufs=3))
         wbf_pool = ctx.enter_context(tc.tile_pool(name="wbf", bufs=3))
         grp_pool = ctx.enter_context(tc.tile_pool(name="grp", bufs=2))
         code_pool = ctx.enter_context(tc.tile_pool(name="code", bufs=3))
@@ -171,17 +171,15 @@ def tile_differentialselfattention_pa_kernel(
         x_codes = [const.tile([P, 2, 512], U32, name="x_codes%d" % h, align_bytes=64) for h in range(2)]
         x_scales = [const.tile([P, 2, 512], U8, name="x_scales%d" % h, align_bytes=64) for h in range(2)]
 
-        def widen(wide, c, s, on_vector):
-            if on_vector:
-                nc.vector.tensor_tensor(
-                    out=wide[:, s, :], in0=wq_bytes[c][:, s, :].bitcast(FP8), in1=sc_bc[:], op=ALU.mult
-                )
-            else:
-                cast = cast_pool.tile([P, D], BF16, tag="cast")
+        def widen(wide, c, s, on_gpsimd):
+            cast = cast_pool.tile([P, D], BF16, tag="cast")
+            if not on_gpsimd:
                 nc.scalar.copy(out=cast[:], in_=wq_bytes[c][:, s, :].bitcast(FP8))
-                for j in range(2):
-                    cols = slice(512 * j, 512 * (j + 1))
-                    nc.gpsimd.tensor_tensor(out=wide[:, s, cols], in0=cast[:, cols], in1=sc_bc[:, cols], op=ALU.mult)
+            for j in range(2):
+                cols = slice(512 * j, 512 * (j + 1))
+                if on_gpsimd:
+                    nc.gpsimd.tensor_copy(out=cast[:, cols], in_=wq_bytes[c][:, s, cols].bitcast(FP8))
+                nc.gpsimd.tensor_tensor(out=wide[:, s, cols], in0=cast[:, cols], in1=sc_bc[:, cols], op=ALU.mult)
 
         def project(c, h, wcs):
             codes, scales = wcs
@@ -276,9 +274,9 @@ def tile_differentialselfattention_pa_kernel(
         tile_no = 0
         for b in range(11):
             widen_plan[b] = []
-            for on_vector in ((False, True) if b % 2 == 0 and b < 10 else (False,)):
+            for on_gpsimd in ((False, True) if b % 2 == 0 and b < 10 else (False,)):
                 if tile_no < 16:
-                    widen_plan[b].append((tile_no // 4, tile_no % 4, on_vector))
+                    widen_plan[b].append((tile_no // 4, tile_no % 4, on_gpsimd))
                     tile_no += 1
 
         def prep_job(b, j):
@@ -301,11 +299,11 @@ def tile_differentialselfattention_pa_kernel(
             prep_job(n, 0)
             turn_back(terms[1], rot, 1)
             prep_job(n, 1)
-            for cq, s, on_vector in widen_plan.get(n, []):
+            for cq, s, on_gpsimd in widen_plan.get(n, []):
                 if s == 0:
                     wide = wbf_pool.tile([P, 4, D], BF16, tag="wbf")
                     wides[cq] = wide
-                widen(wides[cq], cq, s, on_vector)
+                widen(wides[cq], cq, s, on_gpsimd)
             turn_back(terms[2], rot, 2)
             if n == 15:
                 store(c, h, rot, [0])

@@ -142,12 +142,16 @@ def tile_differentialselfattention_pa_kernel(
             nc.tensor.transpose(pb[:], brow[:], ident_b[:])
             nc.vector.tensor_copy(out=bias_f[:], in_=pb[:, 0:32])
 
-        def turn_rows(rows, s, grouped, on_vector):
+        def turn_rows(rows, s, grouped, on_vector, sorted_words=False):
             words = rows[:, s, :].bitcast(F32)
             pin = psum_tp.tile([P, 2, 2, P], F32, tag="tp")
             for g in range(2):
                 for u in range(2):
-                    nc.tensor.transpose(pin[:, g, u, :], words[:, 256 * g + u:256 * (g + 1):2], ident_f[:])
+                    if sorted_words:
+                        picked = words[:, 256 * g + P * u:256 * g + P * (u + 1)]
+                    else:
+                        picked = words[:, 256 * g + u:256 * (g + 1):2]
+                    nc.tensor.transpose(pin[:, g, u, :], picked, ident_f[:])
             out_of_psum(
                 on_vector, grouped[:, :, P * s:P * (s + 1), :].bitcast(F32), pin[:].rearrange("p g u r -> p g r u")
             )
@@ -179,7 +183,12 @@ def tile_differentialselfattention_pa_kernel(
                 cols = slice(512 * j, 512 * (j + 1))
                 if on_gpsimd:
                     nc.gpsimd.tensor_copy(out=cast[:, cols], in_=wq_bytes[c][:, s, cols].bitcast(FP8))
-                nc.gpsimd.tensor_tensor(out=wide[:, s, cols], in0=cast[:, cols], in1=sc_bc[:, cols], op=ALU.mult)
+                nc.gpsimd.tensor_tensor(
+                    out=wide[:, s, cols].rearrange("p (u w e) -> p w u e", u=2, e=2),
+                    in0=cast[:, cols].rearrange("p (w u e) -> p w u e", u=2, e=2),
+                    in1=sc_bc[:, cols].rearrange("p (w u e) -> p w u e", u=2, e=2),
+                    op=ALU.mult,
+                )
 
         def project(c, h, wcs):
             codes, scales = wcs
@@ -285,7 +294,7 @@ def tile_differentialselfattention_pa_kernel(
             c, s = jobs[2 * b + j]
             if s == 0:
                 groupeds[c] = new_grouped()
-            turn_rows(rows_of(c), s, groupeds[c], False)
+            turn_rows(rows_of(c), s, groupeds[c], False, c < 4)
 
         for n in range(16):
             c, h = units[n]

@@ -61,8 +61,11 @@ def tile_differentialselfattention_pa_kernel(
 
         load_rows(x_half[0], x_view, 0, 4)
         load_rows(wk_rows[0], wk_view, 0, 4)
-        nc.sync.dma_start(out=brow[0:16, :], in_=bq.rearrange("(r c) -> r c", c=P))
-        nc.sync.dma_start(out=brow[16:32, :], in_=bk.rearrange("(r c) -> r c", c=P))
+        for b, vec in enumerate((bq, bk)):
+            halves = vec.rearrange("(m e f i) -> f m e i", e=2, f=2, i=HALF)
+            for f in range(2):
+                rows = slice(16 * b + 8 * f, 16 * b + 8 * (f + 1))
+                nc.sync.dma_start(out=brow[rows, :].rearrange("m (e i) -> m e i", e=2), in_=halves[f])
         load_rows(x_half[1], x_view, 4, 2)
         load_rows(wk_rows[1], wk_view, 4, 2)
         nc.sync.dma_start(out=sc_bc[:], in_=Wq_scale.rearrange("o k -> (o k)").partition_broadcast(P))
@@ -79,13 +82,10 @@ def tile_differentialselfattention_pa_kernel(
         nc.scalar.activation(out=warm[:], in_=zero1[:], func=ACT.Sin)
 
         ident_f = const.tile([P, P], F32, name="ident_f")
-        swap_f = const.tile([P, P], F32, name="swap_f")
         ident_b = const.tile([P, P], BF16, name="ident_b")
         tok_f = const.tile([P, 8], F32, name="tok_f")
         make_identity(nc, ident_f[:])
         nc.gpsimd.iota(tok_f[:], pattern=[[1, 8]], base=0, channel_multiplier=8, allow_small_or_imprecise_dtypes=True)
-        nc.gpsimd.tensor_copy(out=swap_f[:, 0:HALF], in_=ident_f[:, HALF:P])
-        nc.gpsimd.tensor_copy(out=swap_f[:, HALF:P], in_=ident_f[:, 0:HALF])
         make_identity(nc, ident_b[:])
 
         freq = const.tile([P, HALF], F32, name="freq")
@@ -116,14 +116,14 @@ def tile_differentialselfattention_pa_kernel(
         nc.vector.tensor_scalar(out=ac2, in0=ac2, scalar1=0.5 * math.pi, scalar2=None, op0=ALU.add)
 
         tab_rows = const.tile([P, 8, 2, P], F32, name="tab_rows")
-        tab_cols = const.tile([P, 2, 2, 512], F32, name="tab_cols")
+        tab_cols = const.tile([P, 3, 2, 512], F32, name="tab_cols")
         bias_f = const.tile([P, 32], F32, name="bias_f")
 
         def sines():
             nc.scalar.activation(out=tab_rows[:, :, 0, 0:HALF], in_=ang_c[:], func=ACT.Sin)
             nc.scalar.activation(out=tab_rows[:, :, 0, HALF:P], in_=ang_c[:], func=ACT.Sin)
             nc.scalar.activation(out=tab_rows[:, :, 1, 0:HALF], in_=ang_s[:], func=ACT.Sin)
-            nc.scalar.activation(out=tab_rows[:, :, 1, HALF:P], in_=ang_s[:], func=ACT.Sin, scale=-1.0)
+            nc.scalar.activation(out=tab_rows[:, :, 1, HALF:P], in_=ang_s[:], func=ACT.Sin)
 
         def out_of_psum(on_vector, out, in_):
             if on_vector:
@@ -135,14 +135,17 @@ def tile_differentialselfattention_pa_kernel(
             bank = psum_tp.tile([P, 4, P], F32, tag="tp")
             for al in range(4):
                 nc.tensor.transpose(bank[:, al, :], tab_rows[:, 4 * h + al, o, :], ident_f[:])
-            out_of_psum(on_vector, tab_cols[:, o, h, :], bank[:].rearrange("p a r -> p (a r)"))
+            flat = bank[:].rearrange("p a r -> p (a r)")
+            out_of_psum(on_vector, tab_cols[:, o + 1, h, :], flat)
+            if o == 1:
+                nc.scalar.mul(out=tab_cols[:, 0, h, :], in_=flat, mul=-1.0)
 
         def turn_bias():
             pb = psum_tp.tile([P, P], BF16, tag="tp")
             nc.tensor.transpose(pb[:], brow[:], ident_b[:])
             nc.vector.tensor_copy(out=bias_f[:], in_=pb[:, 0:32])
 
-        def turn_rows(rows, s, grouped, on_vector, sorted_words=False):
+        def turn_rows(rows, s, out, on_vector, sorted_words=False):
             words = rows[:, s, :].bitcast(F32)
             pin = psum_tp.tile([P, 2, 2, P], F32, tag="tp")
             for g in range(2):
@@ -151,10 +154,20 @@ def tile_differentialselfattention_pa_kernel(
                         picked = words[:, 256 * g + P * u:256 * g + P * (u + 1)]
                     else:
                         picked = words[:, 256 * g + u:256 * (g + 1):2]
-                    nc.tensor.transpose(pin[:, g, u, :], picked, ident_f[:])
-            out_of_psum(
-                on_vector, grouped[:, :, P * s:P * (s + 1), :].bitcast(F32), pin[:].rearrange("p g u r -> p g r u")
-            )
+                    nc.tensor.transpose(pin[:, u, g, :], picked, ident_f[:])
+            if out.shape[1] == 4:
+                view = pin[:].rearrange("p u g (f i) -> p (g f) i u", f=2)
+            else:
+                view = pin[:].rearrange("p u g r -> p g r u")
+            out_of_psum(on_vector, out, view)
+
+        def x_columns(grouped, s):
+            return grouped[:, :, P * s:P * (s + 1), :].bitcast(F32)
+
+        def w_columns(grouped, s):
+            words = grouped[:].rearrange("p a r t -> p (a r t)").bitcast(F32)
+            words = words.rearrange("p (j b e i u) -> p j b e i u", j=2, b=4, e=2, u=2)
+            return words[:, s // 2, :, s % 2, :, :]
 
         def new_grouped():
             grouped = grp_pool.tile([P, 2, 512, 4], BF16, tag="grouped", align_bytes=64)
@@ -193,47 +206,63 @@ def tile_differentialselfattention_pa_kernel(
         def project(c, h, wcs):
             codes, scales = wcs
             accs = []
-            for s in range(4):
-                acc = psum_mx.tile([P, 512], F32, tag="acc")
-                for g in range(2):
-                    nc.tensor.matmul_mx(
-                        out=acc[:],
-                        lhsT=codes[:, g, P * s:P * (s + 1)].bitcast(FP8X4),
-                        lhsT_scale=scales[:, g, P * s:P * (s + 1)],
-                        rhs=x_codes[h][:, g, :].bitcast(FP8X4),
-                        rhs_scale=x_scales[h][:, g, :],
-                        start=(g == 0),
-                        stop=(g == 1),
-                    )
-                accs.append(acc)
+            for j in range(2):
+                for f in range(2):
+                    acc = psum_mx.tile([P, 512], F32, tag="acc")
+                    for g in range(2):
+                        cols = slice(256 * g + P * f, 256 * g + P * (f + 1))
+                        nc.tensor.matmul_mx(
+                            out=acc[:],
+                            lhsT=codes[:, j, cols].bitcast(FP8X4),
+                            lhsT_scale=scales[:, j, cols],
+                            rhs=x_codes[h][:, g, :].bitcast(FP8X4),
+                            rhs_scale=x_scales[h][:, g, :],
+                            start=(g == 0),
+                            stop=(g == 1),
+                        )
+                    accs.append(acc)
             return accs
 
         def products(c, h, accs):
             terms = []
-            for s in range(4):
-                term = term_pool.tile([P, 2, 512], F32, tag="term")
-                nc.vector.scalar_tensor_tensor(
-                    out=term[:],
-                    in0=accs[s][:].unsqueeze(1).to_broadcast([P, 2, 512]),
-                    scalar=bias_f[:, 4 * c + s:4 * c + s + 1],
-                    in1=tab_cols[:, :, h, :],
-                    op0=ALU.add,
-                    op1=ALU.mult,
-                )
-                terms.append(term)
+            for j in range(2):
+                for f in range(2):
+                    term = term_pool.tile([P, 2, 512], F32, tag="term")
+                    col = 16 * (c // 4) + 8 * f + 2 * (c % 4) + j
+                    nc.vector.scalar_tensor_tensor(
+                        out=term[:],
+                        in0=accs[2 * j + f][:].unsqueeze(1).to_broadcast([P, 2, 512]),
+                        scalar=bias_f[:, col:col + 1],
+                        in1=tab_cols[:, 1 - f:3 - f, h, :],
+                        op0=ALU.add,
+                        op1=ALU.mult,
+                    )
+                    terms.append(term)
             return terms
 
-        def turn_back(term, rot, s):
+        def add_pair(terms, j):
+            nc.gpsimd.tensor_tensor(out=terms[2 * j][:], in0=terms[2 * j][:], in1=terms[2 * j + 1][:], op=ALU.add)
+
+        def turn_back(terms, rot, j, f, added):
             bank = psum_tp.tile([P, 4, P], F32, tag="tp")
             for al in range(4):
                 cols = slice(P * al, P * (al + 1))
-                nc.tensor.matmul(
-                    out=bank[:, al, :], lhsT=term[:, 0, cols], rhs=ident_f[:], is_transpose=True, start=True, stop=False
-                )
-                nc.tensor.matmul(
-                    out=bank[:, al, :], lhsT=term[:, 1, cols], rhs=swap_f[:], is_transpose=True, start=False, stop=True
-                )
-            nc.scalar.copy(out=rot[:, s, :, :], in_=bank[:])
+                if added:
+                    nc.tensor.transpose(bank[:, al, :], terms[2 * j][:, f, cols], ident_f[:])
+                else:
+                    for k in range(2):
+                        nc.tensor.matmul(
+                            out=bank[:, al, :],
+                            lhsT=terms[2 * j + k][:, f, cols],
+                            rhs=ident_f[:],
+                            is_transpose=True,
+                            start=(k == 0),
+                            stop=(k == 1),
+                        )
+            nc.scalar.copy(
+                out=rot[:, 2 * j:2 * j + 2, :, HALF * f:HALF * (f + 1)].rearrange("p e a i -> p a e i"),
+                in_=bank[:].rearrange("p a (e i) -> p a e i", e=2),
+            )
 
         def store(c, h, rot, subs):
             head = 2 * (c % 4)
@@ -253,18 +282,18 @@ def tile_differentialselfattention_pa_kernel(
 
         gx0 = new_grouped()
         for s in range(4):
-            turn_rows(x_half[0], s, gx0, False)
+            turn_rows(x_half[0], s, x_columns(gx0, s), False)
         quantise(gx0, x_codes[0], x_scales[0])
         g0 = new_grouped()
         for s in range(4):
-            turn_rows(rows_of(order[0]), s, g0, s >= 2)
+            turn_rows(rows_of(order[0]), s, w_columns(g0, s), s >= 2)
         wcs[order[0]] = new_codes()
         quantise(g0, wcs[order[0]][0], wcs[order[0]][1])
         sines()
         turn_bias()
         gx1 = new_grouped()
         for s in range(4):
-            turn_rows(x_half[1], s, gx1, s % 2 == 0)
+            turn_rows(x_half[1], s, x_columns(gx1, s), s % 2 == 0)
         quantise(gx1, x_codes[1], x_scales[1])
         accs = project(units[0][0], units[0][1], wcs[units[0][0]])
         for o in range(2):
@@ -274,7 +303,7 @@ def tile_differentialselfattention_pa_kernel(
             turn_table(1, o, False)
         g1 = new_grouped()
         for s in range(4):
-            turn_rows(rows_of(order[1]), s, g1, False)
+            turn_rows(rows_of(order[1]), s, w_columns(g1, s), False)
         wcs[order[1]] = new_codes()
         quantise(g1, wcs[order[1]][0], wcs[order[1]][1])
 
@@ -294,8 +323,13 @@ def tile_differentialselfattention_pa_kernel(
             c, s = jobs[2 * b + j]
             if s == 0:
                 groupeds[c] = new_grouped()
-            turn_rows(rows_of(c), s, groupeds[c], False, c < 4)
+            turn_rows(rows_of(c), s, w_columns(groupeds[c], s), False, c < 4)
 
+        def on_gpsimd_adds(n):
+            return {0: [0], 12: [0, 1], 13: [0, 1], 14: [0, 1], 15: [0]}.get(n, [])
+
+        for j in on_gpsimd_adds(0):
+            add_pair(terms, j)
         for n in range(16):
             c, h = units[n]
             nxt = None
@@ -303,21 +337,21 @@ def tile_differentialselfattention_pa_kernel(
                 c2, h2 = units[n + 1]
                 accs = project(c2, h2, wcs[c2])
                 nxt = products(c2, h2, accs)
+                for j in on_gpsimd_adds(n + 1):
+                    add_pair(nxt, j)
             rot = rot_pool.tile([P, 4, 4, P], F32, tag="rot")
-            turn_back(terms[0], rot, 0)
-            prep_job(n, 0)
-            turn_back(terms[1], rot, 1)
-            prep_job(n, 1)
-            for cq, s, on_gpsimd in widen_plan.get(n, []):
-                if s == 0:
-                    wide = wbf_pool.tile([P, 4, D], BF16, tag="wbf")
-                    wides[cq] = wide
-                widen(wides[cq], cq, s, on_gpsimd)
-            turn_back(terms[2], rot, 2)
-            if n == 15:
-                store(c, h, rot, [0])
-            turn_back(terms[3], rot, 3)
-            store(c, h, rot, [1] if n == 15 else [0, 1])
+            for j in range(2):
+                added = j in on_gpsimd_adds(n)
+                turn_back(terms, rot, j, 0, added)
+                prep_job(n, j)
+                turn_back(terms, rot, j, 1, added)
+                if j == 0:
+                    for cq, s, on_gpsimd in widen_plan.get(n, []):
+                        if s == 0:
+                            wide = wbf_pool.tile([P, 4, D], BF16, tag="wbf")
+                            wides[cq] = wide
+                        widen(wides[cq], cq, s, on_gpsimd)
+            store(c, h, rot, [0, 1])
             if 2 * n + 1 < len(jobs) and jobs[2 * n + 1][1] == 3:
                 cj = jobs[2 * n + 1][0]
                 wcs[cj] = new_codes()

@@ -20,8 +20,6 @@ P = 128
 D = 1024
 HALF = 64
 TWO_PI = 2.0 * math.pi
-PI_HI = 6.28125
-PI_LO = TWO_PI - PI_HI
 
 
 def tile_differentialselfattention_pa_kernel(
@@ -50,7 +48,19 @@ def tile_differentialselfattention_pa_kernel(
         wk_rows = [const.tile([P, 4, D], BF16, name="wk_rows%d" % c) for c in range(4)]
         x_half = [const.tile([P, 4, D], BF16, name="x_half%d" % h) for h in range(2)]
         brow = const.tile([P, P], BF16, name="brow")
+        ident_f = const.tile([P, P], F32, name="ident_f")
+        ident_b = const.tile([P, P], BF16, name="ident_b")
+        tok = const.tile([P, 2, 512], F32, name="tok")
+        make_identity(nc, ident_f[:])
         nc.gpsimd.memset(brow[:], 0.0)
+        nc.gpsimd.iota(
+            tok[:].rearrange("p h (a r) -> p h a r", a=4),
+            pattern=[[4, 2], [1, 4], [8, P]],
+            base=0,
+            channel_multiplier=0,
+            allow_small_or_imprecise_dtypes=True,
+        )
+        make_identity(nc, ident_b[:])
 
         def load_rows(tile, view, first, pieces):
             step = 4 // pieces
@@ -81,71 +91,53 @@ def tile_differentialselfattention_pa_kernel(
         warm = const.tile([P, 1], F32, name="warm")
         nc.scalar.activation(out=warm[:], in_=zero1[:], func=ACT.Sin)
 
-        ident_f = const.tile([P, P], F32, name="ident_f")
-        ident_b = const.tile([P, P], BF16, name="ident_b")
-        tok_f = const.tile([P, 8], F32, name="tok_f")
-        make_identity(nc, ident_f[:])
-        nc.gpsimd.iota(tok_f[:], pattern=[[1, 8]], base=0, channel_multiplier=8, allow_small_or_imprecise_dtypes=True)
-        make_identity(nc, ident_b[:])
-
-        freq = const.tile([P, HALF], F32, name="freq")
+        freq = const.tile([P, P], F32, name="freq")
         nc.vector.memset(freq[:, 0:1], 1.0)
         for w in (1, 2, 4, 8, 16, 32):
             nc.vector.tensor_scalar(
                 out=freq[:, w:2 * w], in0=freq[:, 0:w], scalar1=10000.0 ** (-1.0 * w / HALF), scalar2=None, op0=ALU.mult
             )
-        theta = const.tile([P, 8, HALF], F32, name="theta")
-        nc.vector.tensor_tensor(
-            out=theta[:],
-            in0=tok_f[:].unsqueeze(2).to_broadcast([P, 8, HALF]),
-            in1=freq[:].unsqueeze(1).to_broadcast([P, 8, HALF]),
-            op=ALU.mult,
+        nc.vector.tensor_copy(out=freq[:, HALF:P], in_=freq[:, 0:HALF])
+        f_col = const.tile([P, 1], F32, name="f_col")
+        turned_freq = psum_tp.tile([P, P], F32, tag="tp")
+        nc.tensor.transpose(turned_freq[:], freq[:], ident_f[:])
+        nc.vector.tensor_scalar(
+            out=f_col[:], in0=turned_freq[:, 0:1], scalar1=1.0 / TWO_PI, scalar2=None, op0=ALU.mult
         )
-        th2 = theta[:].rearrange("p a i -> p (a i)")
-        turns_i = const.tile([P, 8 * HALF], I32, name="turns_i")
-        nc.vector.tensor_scalar(out=turns_i[:], in0=th2, scalar1=1.0 / TWO_PI, scalar2=None, op0=ALU.mult)
-        turns = const.tile([P, 8 * HALF], F32, name="turns")
-        nc.vector.tensor_copy(out=turns[:], in_=turns_i[:])
-        ang_s = const.tile([P, 8, HALF], F32, name="ang_s")
-        as2 = ang_s[:].rearrange("p a i -> p (a i)")
-        nc.vector.scalar_tensor_tensor(out=as2, in0=turns[:], scalar=-PI_HI, in1=th2, op0=ALU.mult, op1=ALU.add)
-        nc.vector.scalar_tensor_tensor(out=as2, in0=turns[:], scalar=-PI_LO, in1=as2, op0=ALU.mult, op1=ALU.add)
-        ang_c = const.tile([P, 8, HALF], F32, name="ang_c")
-        ac2 = ang_c[:].rearrange("p a i -> p (a i)")
-        nc.vector.scalar_tensor_tensor(out=ac2, in0=as2, scalar=-1.0, in1=as2, op0=ALU.mult, op1=ALU.min)
-        nc.vector.tensor_scalar(out=ac2, in0=ac2, scalar1=0.5 * math.pi, scalar2=None, op0=ALU.add)
+        quarter = const.tile([P, 1], F32, name="quarter")
+        nc.vector.tensor_scalar(out=quarter[:], in0=zero1[:], scalar1=0.5 * math.pi, scalar2=None, op0=ALU.add)
 
-        tab_rows = const.tile([P, 8, 2, P], F32, name="tab_rows")
-        tab_cols = const.tile([P, 3, 2, 512], F32, name="tab_cols")
+        whole_i = const.tile([P, 2, 512], I32, name="whole_i")
+        whole = const.tile([P, 2, 512], F32, name="whole")
+        part = const.tile([P, 2, 512], F32, name="part")
+        minus_abs = const.tile([P, 2, 512], F32, name="minus_abs")
+
+        def whole_turns(h):
+            nc.vector.tensor_scalar(out=whole_i[:, h, :], in0=tok[:, h, :], scalar1=f_col[:], scalar2=None, op0=ALU.mult)
+            nc.vector.tensor_copy(out=whole[:, h, :], in_=whole_i[:, h, :])
+
+        def parts_of_turns(h):
+            nc.vector.scalar_tensor_tensor(
+                out=part[:, h, :], in0=tok[:, h, :], scalar=f_col[:], in1=whole[:, h, :], op0=ALU.mult, op1=ALU.subtract
+            )
+            nc.vector.scalar_tensor_tensor(
+                out=minus_abs[:, h, :], in0=part[:, h, :], scalar=-1.0, in1=part[:, h, :], op0=ALU.mult, op1=ALU.min
+            )
+
+        table = const.tile([P, 3, 2, 512], F32, name="table")
         bias_f = const.tile([P, 32], F32, name="bias_f")
 
-        def sines():
-            nc.scalar.activation(out=tab_rows[:, :, 0, 0:HALF], in_=ang_c[:], func=ACT.Sin)
-            nc.scalar.activation(out=tab_rows[:, :, 0, HALF:P], in_=ang_c[:], func=ACT.Sin)
-            nc.scalar.activation(out=tab_rows[:, :, 1, 0:HALF], in_=ang_s[:], func=ACT.Sin)
-            nc.scalar.activation(out=tab_rows[:, :, 1, HALF:P], in_=ang_s[:], func=ACT.Sin)
-
-        def out_of_psum(on_vector, out, in_):
-            if on_vector:
-                nc.vector.tensor_copy(out=out, in_=in_)
-            else:
-                nc.scalar.copy(out=out, in_=in_)
-
-        def turn_table(h, o, on_vector):
-            bank = psum_tp.tile([P, 4, P], F32, tag="tp")
-            for al in range(4):
-                nc.tensor.transpose(bank[:, al, :], tab_rows[:, 4 * h + al, o, :], ident_f[:])
-            flat = bank[:].rearrange("p a r -> p (a r)")
-            out_of_psum(on_vector, tab_cols[:, o + 1, h, :], flat)
-            if o == 1:
-                nc.scalar.mul(out=tab_cols[:, 0, h, :], in_=flat, mul=-1.0)
+        def sines(h):
+            nc.scalar.activation(out=table[:, 1, h, :], in_=minus_abs[:, h, :], func=ACT.Sin, scale=TWO_PI, bias=quarter[:])
+            nc.scalar.activation(out=table[:, 2, h, :], in_=part[:, h, :], func=ACT.Sin, scale=TWO_PI)
+            nc.scalar.activation(out=table[:, 0, h, :], in_=part[:, h, :], func=ACT.Sin, scale=-TWO_PI)
 
         def turn_bias():
             pb = psum_tp.tile([P, P], BF16, tag="tp")
             nc.tensor.transpose(pb[:], brow[:], ident_b[:])
             nc.vector.tensor_copy(out=bias_f[:], in_=pb[:, 0:32])
 
-        def turn_rows(rows, s, out, on_vector, sorted_words=False):
+        def turn_rows(rows, s, out, split_halves, sorted_words=False):
             words = rows[:, s, :].bitcast(F32)
             pin = psum_tp.tile([P, 2, 2, P], F32, tag="tp")
             for g in range(2):
@@ -155,30 +147,33 @@ def tile_differentialselfattention_pa_kernel(
                     else:
                         picked = words[:, 256 * g + u:256 * (g + 1):2]
                     nc.tensor.transpose(pin[:, u, g, :], picked, ident_f[:])
-            if out.shape[1] == 4:
+            if split_halves:
                 view = pin[:].rearrange("p u g (f i) -> p (g f) i u", f=2)
             else:
                 view = pin[:].rearrange("p u g r -> p g r u")
-            out_of_psum(on_vector, out, view)
+            nc.scalar.copy(out=out, in_=view)
 
-        def x_columns(grouped, s):
-            return grouped[:, :, P * s:P * (s + 1), :].bitcast(F32)
+        def turn_x(rows, s, grouped):
+            turn_rows(rows, s, grouped[:, :, P * s:P * (s + 1), :].bitcast(F32), False)
 
-        def w_columns(grouped, s):
+        def turn_w(rows, s, grouped, sorted_words=False):
             words = grouped[:].rearrange("p a r t -> p (a r t)").bitcast(F32)
             words = words.rearrange("p (j b e i u) -> p j b e i u", j=2, b=4, e=2, u=2)
-            return words[:, s // 2, :, s % 2, :, :]
+            turn_rows(rows, s, words[:, s // 2, :, s % 2, :, :], True, sorted_words)
 
         def new_grouped():
             grouped = grp_pool.tile([P, 2, 512, 4], BF16, tag="grouped", align_bytes=64)
             return grouped
 
-        def quantise(grouped, codes, scales):
-            nc.vector.quantize_mx(
-                out=codes[:].rearrange("p g c -> p (g c)").bitcast(FP8X4),
-                scales=scales[:].rearrange("p g c -> p (g c)"),
-                in_=grouped[:].rearrange("p g r t -> p (g r t)"),
-            )
+        def quantise(grouped, codes, scales, parts=1):
+            step = 2 // parts
+            for k in range(parts):
+                part = slice(step * k, step * (k + 1))
+                nc.vector.quantize_mx(
+                    out=codes[:, part, :].rearrange("p g c -> p (g c)").bitcast(FP8X4),
+                    scales=scales[:, part, :].rearrange("p g c -> p (g c)"),
+                    in_=grouped[:, part, :, :].rearrange("p g r t -> p (g r t)"),
+                )
 
         def new_codes():
             codes = code_pool.tile([P, 2, 512], U32, tag="wcodes", align_bytes=64)
@@ -188,14 +183,11 @@ def tile_differentialselfattention_pa_kernel(
         x_codes = [const.tile([P, 2, 512], U32, name="x_codes%d" % h, align_bytes=64) for h in range(2)]
         x_scales = [const.tile([P, 2, 512], U8, name="x_scales%d" % h, align_bytes=64) for h in range(2)]
 
-        def widen(wide, c, s, on_gpsimd):
+        def widen(wide, c, s):
             cast = cast_pool.tile([P, D], BF16, tag="cast")
-            if not on_gpsimd:
-                nc.scalar.copy(out=cast[:], in_=wq_bytes[c][:, s, :].bitcast(FP8))
+            nc.scalar.copy(out=cast[:], in_=wq_bytes[c][:, s, :].bitcast(FP8))
             for j in range(2):
                 cols = slice(512 * j, 512 * (j + 1))
-                if on_gpsimd:
-                    nc.gpsimd.tensor_copy(out=cast[:, cols], in_=wq_bytes[c][:, s, cols].bitcast(FP8))
                 nc.gpsimd.tensor_tensor(
                     out=wide[:, s, cols].rearrange("p (u w e) -> p w u e", u=2, e=2),
                     in0=cast[:, cols].rearrange("p (w u e) -> p w u e", u=2, e=2),
@@ -203,42 +195,37 @@ def tile_differentialselfattention_pa_kernel(
                     op=ALU.mult,
                 )
 
-        def project(c, h, wcs):
+        def project(h, wcs, j):
             codes, scales = wcs
             accs = []
-            for j in range(2):
-                for f in range(2):
-                    acc = psum_mx.tile([P, 512], F32, tag="acc")
-                    for g in range(2):
-                        cols = slice(256 * g + P * f, 256 * g + P * (f + 1))
-                        nc.tensor.matmul_mx(
-                            out=acc[:],
-                            lhsT=codes[:, j, cols].bitcast(FP8X4),
-                            lhsT_scale=scales[:, j, cols],
-                            rhs=x_codes[h][:, g, :].bitcast(FP8X4),
-                            rhs_scale=x_scales[h][:, g, :],
-                            start=(g == 0),
-                            stop=(g == 1),
-                        )
-                    accs.append(acc)
+            for f in range(2):
+                acc = psum_mx.tile([P, 512], F32, tag="acc")
+                for g in range(2):
+                    cols = slice(256 * g + P * f, 256 * g + P * (f + 1))
+                    nc.tensor.matmul_mx(
+                        out=acc[:],
+                        lhsT=codes[:, j, cols].bitcast(FP8X4),
+                        lhsT_scale=scales[:, j, cols],
+                        rhs=x_codes[h][:, g, :].bitcast(FP8X4),
+                        rhs_scale=x_scales[h][:, g, :],
+                        start=(g == 0),
+                        stop=(g == 1),
+                    )
+                accs.append(acc)
             return accs
 
-        def products(c, h, accs):
-            terms = []
-            for j in range(2):
-                for f in range(2):
-                    term = term_pool.tile([P, 2, 512], F32, tag="term")
-                    col = 16 * (c // 4) + 8 * f + 2 * (c % 4) + j
-                    nc.vector.scalar_tensor_tensor(
-                        out=term[:],
-                        in0=accs[2 * j + f][:].unsqueeze(1).to_broadcast([P, 2, 512]),
-                        scalar=bias_f[:, col:col + 1],
-                        in1=tab_cols[:, 1 - f:3 - f, h, :],
-                        op0=ALU.add,
-                        op1=ALU.mult,
-                    )
-                    terms.append(term)
-            return terms
+        def product(c, h, j, f, acc):
+            term = term_pool.tile([P, 2, 512], F32, tag="term")
+            col = 16 * (c // 4) + 8 * f + 2 * (c % 4) + j
+            nc.vector.scalar_tensor_tensor(
+                out=term[:],
+                in0=acc[:].unsqueeze(1).to_broadcast([P, 2, 512]),
+                scalar=bias_f[:, col:col + 1],
+                in1=table[:, 1 - f:3 - f, h, :],
+                op0=ALU.add,
+                op1=ALU.mult,
+            )
+            return term
 
         def add_pair(terms, j):
             nc.gpsimd.tensor_tensor(out=terms[2 * j][:], in0=terms[2 * j][:], in1=terms[2 * j + 1][:], op=ALU.add)
@@ -264,11 +251,13 @@ def tile_differentialselfattention_pa_kernel(
                 in_=bank[:].rearrange("p a (e i) -> p a e i", e=2),
             )
 
-        def store(c, h, rot, subs):
-            head = 2 * (c % 4)
-            for sub in subs:
+        def store(c, h, rot, heads):
+            for sub in range(2):
                 nc.sync.dma_start(
-                    out=out_views[2 * (c // 4) + sub][:, head:head + 2, 4 * h:4 * h + 4, :], in_=rot[:, sub::2, :, :]
+                    out=out_views[2 * (c // 4) + sub][
+                        :, 2 * (c % 4) + heads.start:2 * (c % 4) + heads.stop, 4 * h:4 * h + 4, :
+                    ],
+                    in_=rot[:, 2 * heads.start + sub:2 * heads.stop:2, :, :],
                 )
 
         order = [4, 5, 6, 7, 0, 1, 2, 3]
@@ -280,42 +269,42 @@ def tile_differentialselfattention_pa_kernel(
         def rows_of(c):
             return wides[c] if c < 4 else wk_rows[c - 4]
 
+        whole_turns(0)
+        parts_of_turns(0)
+        whole_turns(1)
         gx0 = new_grouped()
         for s in range(4):
-            turn_rows(x_half[0], s, x_columns(gx0, s), False)
+            turn_x(x_half[0], s, gx0)
         quantise(gx0, x_codes[0], x_scales[0])
         g0 = new_grouped()
         for s in range(4):
-            turn_rows(rows_of(order[0]), s, w_columns(g0, s), s >= 2)
+            turn_w(rows_of(order[0]), s, g0)
         wcs[order[0]] = new_codes()
-        quantise(g0, wcs[order[0]][0], wcs[order[0]][1])
-        sines()
+        quantise(g0, wcs[order[0]][0], wcs[order[0]][1], 2)
+        sines(0)
         turn_bias()
+        parts_of_turns(1)
         gx1 = new_grouped()
         for s in range(4):
-            turn_rows(x_half[1], s, x_columns(gx1, s), s % 2 == 0)
+            turn_x(x_half[1], s, gx1)
+        sines(1)
+        accs = [acc for j in range(2) for acc in project(0, wcs[order[0]], j)]
+        terms = [product(order[0], 0, k // 2, k % 2, accs[k]) for k in range(2)]
         quantise(gx1, x_codes[1], x_scales[1])
-        accs = project(units[0][0], units[0][1], wcs[units[0][0]])
-        for o in range(2):
-            turn_table(0, o, o == 0)
-        terms = products(units[0][0], units[0][1], accs)
-        for o in range(2):
-            turn_table(1, o, False)
-        g1 = new_grouped()
+        terms += [product(order[0], 0, k // 2, k % 2, accs[k]) for k in range(2, 4)]
+        groupeds[order[1]] = new_grouped()
         for s in range(4):
-            turn_rows(rows_of(order[1]), s, w_columns(g1, s), False)
-        wcs[order[1]] = new_codes()
-        quantise(g1, wcs[order[1]][0], wcs[order[1]][1])
+            turn_w(rows_of(order[1]), s, groupeds[order[1]])
+        waiting = [order[1]]
 
         jobs = [(order[k], s) for k in range(2, 8) for s in range(4)]
         widen_plan = {}
         tile_no = 0
         for b in range(11):
             widen_plan[b] = []
-            for on_gpsimd in ((False, True) if b % 2 == 0 and b < 10 else (False,)):
-                if tile_no < 16:
-                    widen_plan[b].append((tile_no // 4, tile_no % 4, on_gpsimd))
-                    tile_no += 1
+            for k in range(2 if b % 2 == 0 and b < 10 else 1):
+                widen_plan[b].append((tile_no // 4, tile_no % 4))
+                tile_no += 1
 
         def prep_job(b, j):
             if 2 * b + j >= len(jobs):
@@ -323,37 +312,45 @@ def tile_differentialselfattention_pa_kernel(
             c, s = jobs[2 * b + j]
             if s == 0:
                 groupeds[c] = new_grouped()
-            turn_rows(rows_of(c), s, w_columns(groupeds[c], s), False, c < 4)
+            turn_w(rows_of(c), s, groupeds[c], c < 4)
+            if s == 3:
+                waiting.append(c)
 
-        def on_gpsimd_adds(n):
-            return {0: [0], 12: [0, 1], 13: [0, 1], 14: [0, 1], 15: [0]}.get(n, [])
+        def gpsimd_adds(n):
+            return {0: [0], 4: [0], 8: [0], 12: [0], 13: [0], 14: [0]}.get(n, [])
 
-        for j in on_gpsimd_adds(0):
+        for j in gpsimd_adds(0):
             add_pair(terms, j)
         for n in range(16):
             c, h = units[n]
-            nxt = None
+            for cq, s in widen_plan.get(n, []):
+                if s == 0:
+                    wide = wbf_pool.tile([P, 4, D], BF16, tag="wbf")
+                    wides[cq] = wide
+                widen(wides[cq], cq, s)
+            nxt = []
             if n + 1 < 16:
                 c2, h2 = units[n + 1]
-                accs = project(c2, h2, wcs[c2])
-                nxt = products(c2, h2, accs)
-                for j in on_gpsimd_adds(n + 1):
-                    add_pair(nxt, j)
+                accs = [acc for j in range(2) for acc in project(h2, wcs[c2], j)]
+                for j in range(2):
+                    for f in range(2):
+                        nxt.append(product(c2, h2, j, f, accs[2 * j + f]))
+                    if j == 0 and waiting:
+                        cw = waiting[0]
+                        waiting.clear()
+                        wcs[cw] = new_codes()
+                        quantise(groupeds[cw], wcs[cw][0], wcs[cw][1])
+                    if j in gpsimd_adds(n + 1):
+                        add_pair(nxt, j)
             rot = rot_pool.tile([P, 4, 4, P], F32, tag="rot")
-            for j in range(2):
-                added = j in on_gpsimd_adds(n)
-                turn_back(terms, rot, j, 0, added)
-                prep_job(n, j)
-                turn_back(terms, rot, j, 1, added)
-                if j == 0:
-                    for cq, s, on_gpsimd in widen_plan.get(n, []):
-                        if s == 0:
-                            wide = wbf_pool.tile([P, 4, D], BF16, tag="wbf")
-                            wides[cq] = wide
-                        widen(wides[cq], cq, s, on_gpsimd)
-            store(c, h, rot, [0, 1])
-            if 2 * n + 1 < len(jobs) and jobs[2 * n + 1][1] == 3:
-                cj = jobs[2 * n + 1][0]
-                wcs[cj] = new_codes()
-                quantise(groupeds[cj], wcs[cj][0], wcs[cj][1])
+            pairs = [1, 0] if gpsimd_adds(n) == [0] else [0, 1]
+            for k in range(2):
+                for f in range(2):
+                    turn_back(terms, rot, pairs[k], f, pairs[k] in gpsimd_adds(n))
+                    if k == 0:
+                        prep_job(n, f)
+                if n == 15:
+                    store(c, h, rot, slice(pairs[k], pairs[k] + 1))
+            if n < 15:
+                store(c, h, rot, slice(0, 2))
             terms = nxt

@@ -183,11 +183,14 @@ def tile_differentialselfattention_pa_kernel(
         x_codes = [const.tile([P, 2, 512], U32, name="x_codes%d" % h, align_bytes=64) for h in range(2)]
         x_scales = [const.tile([P, 2, 512], U8, name="x_scales%d" % h, align_bytes=64) for h in range(2)]
 
-        def widen(wide, c, s):
+        def widen(wide, c, s, cast_on_gpsimd):
             cast = cast_pool.tile([P, D], BF16, tag="cast")
-            nc.scalar.copy(out=cast[:], in_=wq_bytes[c][:, s, :].bitcast(FP8))
+            if not cast_on_gpsimd:
+                nc.scalar.copy(out=cast[:], in_=wq_bytes[c][:, s, :].bitcast(FP8))
             for j in range(2):
                 cols = slice(512 * j, 512 * (j + 1))
+                if cast_on_gpsimd:
+                    nc.gpsimd.tensor_copy(out=cast[:, cols], in_=wq_bytes[c][:, s, cols].bitcast(FP8))
                 nc.gpsimd.tensor_tensor(
                     out=wide[:, s, cols].rearrange("p (u w e) -> p w u e", u=2, e=2),
                     in0=cast[:, cols].rearrange("p (w u e) -> p w u e", u=2, e=2),
@@ -303,7 +306,7 @@ def tile_differentialselfattention_pa_kernel(
         for b in range(11):
             widen_plan[b] = []
             for k in range(2 if b % 2 == 0 and b < 10 else 1):
-                widen_plan[b].append((tile_no // 4, tile_no % 4))
+                widen_plan[b].append((tile_no // 4, tile_no % 4, k == 1))
                 tile_no += 1
 
         def prep_job(b, j):
@@ -317,17 +320,12 @@ def tile_differentialselfattention_pa_kernel(
                 waiting.append(c)
 
         def gpsimd_adds(n):
-            return {0: [0], 4: [0], 8: [0], 12: [0], 13: [0], 14: [0]}.get(n, [])
+            return {0: [0], 12: [0], 13: [0], 14: [0]}.get(n, [])
 
         for j in gpsimd_adds(0):
             add_pair(terms, j)
         for n in range(16):
             c, h = units[n]
-            for cq, s in widen_plan.get(n, []):
-                if s == 0:
-                    wide = wbf_pool.tile([P, 4, D], BF16, tag="wbf")
-                    wides[cq] = wide
-                widen(wides[cq], cq, s)
             nxt = []
             if n + 1 < 16:
                 c2, h2 = units[n + 1]
@@ -349,6 +347,12 @@ def tile_differentialselfattention_pa_kernel(
                     turn_back(terms, rot, pairs[k], f, pairs[k] in gpsimd_adds(n))
                     if k == 0:
                         prep_job(n, f)
+                if k == 0:
+                    for cq, s, cast_on_gpsimd in widen_plan.get(n, []):
+                        if s == 0:
+                            wide = wbf_pool.tile([P, 4, D], BF16, tag="wbf")
+                            wides[cq] = wide
+                        widen(wides[cq], cq, s, cast_on_gpsimd)
                 if n == 15:
                     store(c, h, rot, slice(pairs[k], pairs[k] + 1))
             if n < 15:

@@ -51,8 +51,8 @@ def tile_differentialselfattention_pa_kernel(
         ident_f = const.tile([P, P], F32, name="ident_f")
         ident_b = const.tile([P, P], BF16, name="ident_b")
         tok = const.tile([P, 2, 512], F32, name="tok")
-        make_identity(nc, ident_f[:])
         nc.gpsimd.memset(brow[:], 0.0)
+        make_identity(nc, ident_f[:])
         nc.gpsimd.iota(
             tok[:].rearrange("p h (a r) -> p h a r", a=4),
             pattern=[[4, 2], [1, 4], [8, P]],
@@ -69,13 +69,13 @@ def tile_differentialselfattention_pa_kernel(
                     out=tile[:, step * j:step * (j + 1), :], in_=view[:, first + step * j:first + step * (j + 1), :]
                 )
 
-        load_rows(x_half[0], x_view, 0, 4)
-        load_rows(wk_rows[0], wk_view, 0, 4)
         for b, vec in enumerate((bq, bk)):
             halves = vec.rearrange("(m e f i) -> f m e i", e=2, f=2, i=HALF)
             for f in range(2):
                 rows = slice(16 * b + 8 * f, 16 * b + 8 * (f + 1))
-                nc.sync.dma_start(out=brow[rows, :].rearrange("m (e i) -> m e i", e=2), in_=halves[f])
+                nc.scalar.dma_start(out=brow[rows, :].rearrange("m (e i) -> m e i", e=2), in_=halves[f])
+        load_rows(x_half[0], x_view, 0, 4)
+        load_rows(wk_rows[0], wk_view, 0, 4)
         load_rows(x_half[1], x_view, 4, 2)
         load_rows(wk_rows[1], wk_view, 4, 2)
         nc.sync.dma_start(out=sc_bc[:], in_=Wq_scale.rearrange("o k -> (o k)").partition_broadcast(P))
@@ -183,16 +183,18 @@ def tile_differentialselfattention_pa_kernel(
         x_codes = [const.tile([P, 2, 512], U32, name="x_codes%d" % h, align_bytes=64) for h in range(2)]
         x_scales = [const.tile([P, 2, 512], U8, name="x_scales%d" % h, align_bytes=64) for h in range(2)]
 
-        def widen(wide, c, s, cast_on_gpsimd):
+        wides = {}
+
+        def widen(c, s):
+            if s == 0:
+                wide = wbf_pool.tile([P, 4, D], BF16, tag="wbf")
+                wides[c] = wide
             cast = cast_pool.tile([P, D], BF16, tag="cast")
-            if not cast_on_gpsimd:
-                nc.scalar.copy(out=cast[:], in_=wq_bytes[c][:, s, :].bitcast(FP8))
+            nc.scalar.copy(out=cast[:], in_=wq_bytes[c][:, s, :].bitcast(FP8))
             for j in range(2):
                 cols = slice(512 * j, 512 * (j + 1))
-                if cast_on_gpsimd:
-                    nc.gpsimd.tensor_copy(out=cast[:, cols], in_=wq_bytes[c][:, s, cols].bitcast(FP8))
                 nc.gpsimd.tensor_tensor(
-                    out=wide[:, s, cols].rearrange("p (u w e) -> p w u e", u=2, e=2),
+                    out=wides[c][:, s, cols].rearrange("p (u w e) -> p w u e", u=2, e=2),
                     in0=cast[:, cols].rearrange("p (w u e) -> p w u e", u=2, e=2),
                     in1=sc_bc[:, cols].rearrange("p (w u e) -> p w u e", u=2, e=2),
                     op=ALU.mult,
@@ -230,8 +232,8 @@ def tile_differentialselfattention_pa_kernel(
             )
             return term
 
-        def add_pair(terms, j):
-            nc.gpsimd.tensor_tensor(out=terms[2 * j][:], in0=terms[2 * j][:], in1=terms[2 * j + 1][:], op=ALU.add)
+        def add_pair(engine, terms, j):
+            engine.tensor_tensor(out=terms[2 * j][:], in0=terms[2 * j][:], in1=terms[2 * j + 1][:], op=ALU.add)
 
         def turn_back(terms, rot, j, f, added):
             bank = psum_tp.tile([P, 4, P], F32, tag="tp")
@@ -265,7 +267,6 @@ def tile_differentialselfattention_pa_kernel(
 
         order = [4, 5, 6, 7, 0, 1, 2, 3]
         units = [(c, h) for c in order for h in range(2)]
-        wides = {}
         groupeds = {}
         wcs = {}
 
@@ -301,13 +302,9 @@ def tile_differentialselfattention_pa_kernel(
         waiting = [order[1]]
 
         jobs = [(order[k], s) for k in range(2, 8) for s in range(4)]
-        widen_plan = {}
-        tile_no = 0
-        for b in range(11):
-            widen_plan[b] = []
-            for k in range(2 if b % 2 == 0 and b < 10 else 1):
-                widen_plan[b].append((tile_no // 4, tile_no % 4, k == 1))
-                tile_no += 1
+        widen_first = {b: divmod(3 * b // 2, 4) for b in range(0, 10, 2)}
+        widen_second = {b: divmod((3 * b + 1) // 2 + (b + 1) % 2, 4) for b in range(10)}
+        widen_second[10] = (3, 3)
 
         def prep_job(b, j):
             if 2 * b + j >= len(jobs):
@@ -319,40 +316,37 @@ def tile_differentialselfattention_pa_kernel(
             if s == 3:
                 waiting.append(c)
 
-        def gpsimd_adds(n):
-            return {0: [0], 12: [0], 13: [0], 14: [0]}.get(n, [])
+        adders = {n: nc.gpsimd for n in (0, 4, 8, 12, 13, 14)}
+        for n in (2, 6, 10):
+            adders[n] = nc.vector
 
-        for j in gpsimd_adds(0):
-            add_pair(terms, j)
+        add_pair(adders[0], terms, 0)
         for n in range(16):
             c, h = units[n]
+            if n in widen_first:
+                widen(widen_first[n][0], widen_first[n][1])
             nxt = []
             if n + 1 < 16:
                 c2, h2 = units[n + 1]
                 accs = [acc for j in range(2) for acc in project(h2, wcs[c2], j)]
-                for j in range(2):
-                    for f in range(2):
-                        nxt.append(product(c2, h2, j, f, accs[2 * j + f]))
-                    if j == 0 and waiting:
+                for k in range(4):
+                    nxt.append(product(c2, h2, k // 2, k % 2, accs[k]))
+                    if k == 1 and waiting:
                         cw = waiting[0]
                         waiting.clear()
                         wcs[cw] = new_codes()
                         quantise(groupeds[cw], wcs[cw][0], wcs[cw][1])
-                    if j in gpsimd_adds(n + 1):
-                        add_pair(nxt, j)
+                    if k == 2 and n + 1 in adders:
+                        add_pair(adders[n + 1], nxt, 0)
             rot = rot_pool.tile([P, 4, 4, P], F32, tag="rot")
-            pairs = [1, 0] if gpsimd_adds(n) == [0] else [0, 1]
+            pairs = [1, 0] if n in adders else [0, 1]
             for k in range(2):
                 for f in range(2):
-                    turn_back(terms, rot, pairs[k], f, pairs[k] in gpsimd_adds(n))
+                    turn_back(terms, rot, pairs[k], f, pairs[k] == 0 and n in adders)
                     if k == 0:
                         prep_job(n, f)
-                if k == 0:
-                    for cq, s, cast_on_gpsimd in widen_plan.get(n, []):
-                        if s == 0:
-                            wide = wbf_pool.tile([P, 4, D], BF16, tag="wbf")
-                            wides[cq] = wide
-                        widen(wides[cq], cq, s, cast_on_gpsimd)
+                if k == 0 and n in widen_second:
+                    widen(widen_second[n][0], widen_second[n][1])
                 if n == 15:
                     store(c, h, rot, slice(pairs[k], pairs[k] + 1))
             if n < 15:

@@ -185,12 +185,15 @@ def tile_differentialselfattention_pa_kernel(
 
         wides = {}
 
-        def widen(c, s):
+        def widen(c, s, cast_on_vector):
             if s == 0:
                 wide = wbf_pool.tile([P, 4, D], BF16, tag="wbf")
                 wides[c] = wide
             cast = cast_pool.tile([P, D], BF16, tag="cast")
-            nc.scalar.copy(out=cast[:], in_=wq_bytes[c][:, s, :].bitcast(FP8))
+            if cast_on_vector:
+                nc.vector.tensor_copy(out=cast[:], in_=wq_bytes[c][:, s, :].bitcast(FP8))
+            else:
+                nc.scalar.copy(out=cast[:], in_=wq_bytes[c][:, s, :].bitcast(FP8))
             for j in range(2):
                 cols = slice(512 * j, 512 * (j + 1))
                 nc.gpsimd.tensor_tensor(
@@ -235,26 +238,25 @@ def tile_differentialselfattention_pa_kernel(
         def add_pair(engine, terms, j):
             engine.tensor_tensor(out=terms[2 * j][:], in0=terms[2 * j][:], in1=terms[2 * j + 1][:], op=ALU.add)
 
-        def turn_back(terms, rot, j, f, added):
-            bank = psum_tp.tile([P, 4, P], F32, tag="tp")
-            for al in range(4):
-                cols = slice(P * al, P * (al + 1))
-                if added:
-                    nc.tensor.transpose(bank[:, al, :], terms[2 * j][:, f, cols], ident_f[:])
-                else:
-                    for k in range(2):
-                        nc.tensor.matmul(
-                            out=bank[:, al, :],
-                            lhsT=terms[2 * j + k][:, f, cols],
-                            rhs=ident_f[:],
-                            is_transpose=True,
-                            start=(k == 0),
-                            stop=(k == 1),
-                        )
-            nc.scalar.copy(
-                out=rot[:, 2 * j:2 * j + 2, :, HALF * f:HALF * (f + 1)].rearrange("p e a i -> p a e i"),
-                in_=bank[:].rearrange("p a (e i) -> p a e i", e=2),
-            )
+        def turn_back(terms, rot, j, b, added):
+            bank = psum_tp.tile([P, 2, 2, P], F32, tag="tp")
+            for a in range(2):
+                cols = slice(P * (2 * b + a), P * (2 * b + a + 1))
+                for f in range(2):
+                    out = bank[:, :, a, HALF * f:HALF * (f + 1)]
+                    if added:
+                        nc.tensor.transpose(out, terms[2 * j][:, f, cols], ident_f[:])
+                    else:
+                        for k in range(2):
+                            nc.tensor.matmul(
+                                out=out,
+                                lhsT=terms[2 * j + k][:, f, cols],
+                                rhs=ident_f[:],
+                                is_transpose=True,
+                                start=(k == 0),
+                                stop=(k == 1),
+                            )
+            nc.scalar.copy(out=rot[:, 2 * j:2 * j + 2, 2 * b:2 * b + 2, :], in_=bank[:])
 
         def store(c, h, rot, heads):
             for sub in range(2):
@@ -302,9 +304,15 @@ def tile_differentialselfattention_pa_kernel(
         waiting = [order[1]]
 
         jobs = [(order[k], s) for k in range(2, 8) for s in range(4)]
-        widen_first = {b: divmod(3 * b // 2, 4) for b in range(0, 10, 2)}
-        widen_second = {b: divmod((3 * b + 1) // 2 + (b + 1) % 2, 4) for b in range(10)}
-        widen_second[10] = (3, 3)
+        widen_at_start = {}
+        widen_in_middle = {}
+        tile_no = 0
+        for b in range(11):
+            if b % 2 == 1:
+                widen_at_start[b] = divmod(tile_no, 4)
+                tile_no += 1
+            widen_in_middle[b] = divmod(tile_no, 4)
+            tile_no += 1
 
         def prep_job(b, j):
             if 2 * b + j >= len(jobs):
@@ -316,15 +324,15 @@ def tile_differentialselfattention_pa_kernel(
             if s == 3:
                 waiting.append(c)
 
-        adders = {n: nc.gpsimd for n in (0, 4, 8, 12, 13, 14)}
+        adders = {n: nc.gpsimd for n in (0, 5, 9, 12, 13, 14)}
         for n in (2, 6, 10):
             adders[n] = nc.vector
 
         add_pair(adders[0], terms, 0)
         for n in range(16):
             c, h = units[n]
-            if n in widen_first:
-                widen(widen_first[n][0], widen_first[n][1])
+            if n in widen_at_start:
+                widen(widen_at_start[n][0], widen_at_start[n][1], True)
             nxt = []
             if n + 1 < 16:
                 c2, h2 = units[n + 1]
@@ -345,8 +353,8 @@ def tile_differentialselfattention_pa_kernel(
                     turn_back(terms, rot, pairs[k], f, pairs[k] == 0 and n in adders)
                     if k == 0:
                         prep_job(n, f)
-                if k == 0 and n in widen_second:
-                    widen(widen_second[n][0], widen_second[n][1])
+                if k == 0 and n in widen_in_middle:
+                    widen(widen_in_middle[n][0], widen_in_middle[n][1], False)
                 if n == 15:
                     store(c, h, rot, slice(pairs[k], pairs[k] + 1))
             if n < 15:

from contextlib import ExitStack
import math

import concourse.mybir as mybir
from concourse.masks import make_identity

FLOPS = 2 * 1024 * 1024 * 4096

F32 = mybir.dt.float32
BF16 = mybir.dt.bfloat16
I32 = mybir.dt.int32
U32 = mybir.dt.uint32
U8 = mybir.dt.uint8
FP8 = mybir.dt.float8_e4m3fn
FP8X4 = mybir.dt.float8_e4m3fn_x4
ALU = mybir.AluOpType
ACT = mybir.ActivationFunctionType

P = 128
D = 1024
HALF = 64
TWO_PI = 2.0 * math.pi


def tile_differentialselfattention_pa_kernel(
    tc, x, Wq_bytes, Wq_scale, bq, Wk, bk, out_0, out_1, out_2, out_3
):
    nc = tc.nc
    with ExitStack() as ctx:
        const = ctx.enter_context(tc.tile_pool(name="const", bufs=1))
        cast_pool = ctx.enter_context(tc.tile_pool(name="cast", bufs=3))
        wbf_pool = ctx.enter_context(tc.tile_pool(name="wbf", bufs=3))
        grp_pool = ctx.enter_context(tc.tile_pool(name="grp", bufs=2))
        code_pool = ctx.enter_context(tc.tile_pool(name="code", bufs=3))
        term_pool = ctx.enter_context(tc.tile_pool(name="term", bufs=8))
        rot_pool = ctx.enter_context(tc.tile_pool(name="rot", bufs=3))
        psum_tp = ctx.enter_context(tc.psum_pool(name="psum_tp", bufs=4))
        psum_mx = ctx.enter_context(tc.psum_pool(name="psum_mx", bufs=4))
        ctx.enter_context(tc.manual_schedule())

        wq_view = Wq_bytes.rearrange("(c p) k -> p c k", p=P)
        wk_view = Wk.rearrange("(c p) k -> p c k", p=P)
        x_view = x.rearrange("b (p a) k -> p (b a) k", a=8)
        out_views = [o.rearrange("b h (p a) f -> p (b h) a f", a=8) for o in (out_0, out_1, out_2, out_3)]

        sc_bc = const.tile([P, D], F32, name="sc_bc")
        wq_bytes = [const.tile([P, 4, D], U8, name="wq_bytes%d" % c) for c in range(4)]
        wk_rows = [const.tile([P, 4, D], BF16, name="wk_rows%d" % c) for c in range(4)]
        x_half = [const.tile([P, 4, D], BF16, name="x_half%d" % h) for h in range(2)]
        brow = const.tile([P, P], BF16, name="brow")
        ident_f = const.tile([P, P], F32, name="ident_f")
        ident_b = const.tile([P, P], BF16, name="ident_b")
        tok = const.tile([P, 2, 512], F32, name="tok")
        nc.gpsimd.memset(brow[:], 0.0)
        make_identity(nc, ident_f[:])
        nc.gpsimd.iota(
            tok[:].rearrange("p h (a r) -> p h a r", a=4),
            pattern=[[4, 2], [1, 4], [8, P]],
            base=0,
            channel_multiplier=0,
            allow_small_or_imprecise_dtypes=True,
        )
        make_identity(nc, ident_b[:])

        def load_rows(tile, view, first, pieces):
            step = 4 // pieces
            for j in range(pieces):
                nc.sync.dma_start(
                    out=tile[:, step * j:step * (j + 1), :], in_=view[:, first + step * j:first + step * (j + 1), :]
                )

        for b, vec in enumerate((bq, bk)):
            halves = vec.rearrange("(m e f i) -> f m e i", e=2, f=2, i=HALF)
            for f in range(2):
                rows = slice(16 * b + 8 * f, 16 * b + 8 * (f + 1))
                nc.scalar.dma_start(out=brow[rows, :].rearrange("m (e i) -> m e i", e=2), in_=halves[f])
        load_rows(x_half[0], x_view, 0, 4)
        load_rows(wk_rows[0], wk_view, 0, 4)
        load_rows(x_half[1], x_view, 4, 2)
        load_rows(wk_rows[1], wk_view, 4, 2)
        nc.sync.dma_start(out=sc_bc[:], in_=Wq_scale.rearrange("o k -> (o k)").partition_broadcast(P))
        load_rows(wq_bytes[0], wq_view, 0, 1)
        load_rows(wk_rows[2], wk_view, 8, 1)
        load_rows(wq_bytes[1], wq_view, 4, 1)
        load_rows(wk_rows[3], wk_view, 12, 1)
        load_rows(wq_bytes[2], wq_view, 8, 1)
        load_rows(wq_bytes[3], wq_view, 12, 1)

        zero1 = const.tile([P, 1], F32, name="zero1")
        nc.vector.memset(zero1[:], 0.0)
        warm = const.tile([P, 1], F32, name="warm")
        nc.scalar.activation(out=warm[:], in_=zero1[:], func=ACT.Sin)

        freq = const.tile([P, P], F32, name="freq")
        nc.vector.memset(freq[:, 0:1], 1.0)
        for w in (1, 2, 4, 8, 16, 32):
            nc.vector.tensor_scalar(
                out=freq[:, w:2 * w], in0=freq[:, 0:w], scalar1=10000.0 ** (-1.0 * w / HALF), scalar2=None, op0=ALU.mult
            )
        nc.vector.tensor_copy(out=freq[:, HALF:P], in_=freq[:, 0:HALF])
        f_col = const.tile([P, 1], F32, name="f_col")
        turned_freq = psum_tp.tile([P, P], F32, tag="tp")
        nc.tensor.transpose(turned_freq[:], freq[:], ident_f[:])
        nc.vector.tensor_scalar(
            out=f_col[:], in0=turned_freq[:, 0:1], scalar1=1.0 / TWO_PI, scalar2=None, op0=ALU.mult
        )
        quarter = const.tile([P, 1], F32, name="quarter")
        nc.vector.tensor_scalar(out=quarter[:], in0=zero1[:], scalar1=0.5 * math.pi, scalar2=None, op0=ALU.add)

        whole_i = const.tile([P, 2, 512], I32, name="whole_i")
        whole = const.tile([P, 2, 512], F32, name="whole")
        part = const.tile([P, 2, 512], F32, name="part")
        minus_abs = const.tile([P, 2, 512], F32, name="minus_abs")

        def whole_turns(h):
            nc.vector.tensor_scalar(out=whole_i[:, h, :], in0=tok[:, h, :], scalar1=f_col[:], scalar2=None, op0=ALU.mult)
            nc.vector.tensor_copy(out=whole[:, h, :], in_=whole_i[:, h, :])

        def parts_of_turns(h):
            nc.vector.scalar_tensor_tensor(
                out=part[:, h, :], in0=tok[:, h, :], scalar=f_col[:], in1=whole[:, h, :], op0=ALU.mult, op1=ALU.subtract
            )
            nc.vector.scalar_tensor_tensor(
                out=minus_abs[:, h, :], in0=part[:, h, :], scalar=-1.0, in1=part[:, h, :], op0=ALU.mult, op1=ALU.min
            )

        table = const.tile([P, 3, 2, 512], F32, name="table")
        bias_f = const.tile([P, 32], F32, name="bias_f")

        def sines(h):
            nc.scalar.activation(out=table[:, 1, h, :], in_=minus_abs[:, h, :], func=ACT.Sin, scale=TWO_PI, bias=quarter[:])
            nc.scalar.activation(out=table[:, 2, h, :], in_=part[:, h, :], func=ACT.Sin, scale=TWO_PI)
            nc.scalar.activation(out=table[:, 0, h, :], in_=part[:, h, :], func=ACT.Sin, scale=-TWO_PI)

        def turn_bias():
            pb = psum_tp.tile([P, P], BF16, tag="tp")
            nc.tensor.transpose(pb[:], brow[:], ident_b[:])
            nc.vector.tensor_copy(out=bias_f[:], in_=pb[:, 0:32])

        def turn_rows(rows, s, out, split_halves, sorted_words=False):
            words = rows[:, s, :].bitcast(F32)
            pin = psum_tp.tile([P, 2, 2, P], F32, tag="tp")
            for g in range(2):
                for u in range(2):
                    if sorted_words:
                        picked = words[:, 256 * g + P * u:256 * g + P * (u + 1)]
                    else:
                        picked = words[:, 256 * g + u:256 * (g + 1):2]
                    nc.tensor.transpose(pin[:, u, g, :], picked, ident_f[:])
            if split_halves:
                view = pin[:].rearrange("p u g (f i) -> p (g f) i u", f=2)
            else:
                view = pin[:].rearrange("p u g r -> p g r u")
            nc.scalar.copy(out=out, in_=view)

        def turn_x(rows, s, grouped):
            turn_rows(rows, s, grouped[:, :, P * s:P * (s + 1), :].bitcast(F32), False)

        def turn_w(rows, s, grouped, sorted_words=False):
            words = grouped[:].rearrange("p a r t -> p (a r t)").bitcast(F32)
            words = words.rearrange("p (j b e i u) -> p j b e i u", j=2, b=4, e=2, u=2)
            turn_rows(rows, s, words[:, s // 2, :, s % 2, :, :], True, sorted_words)

        def new_grouped():
            grouped = grp_pool.tile([P, 2, 512, 4], BF16, tag="grouped", align_bytes=64)
            return grouped

        def quantise(grouped, codes, scales, parts=1):
            step = 2 // parts
            for k in range(parts):
                part = slice(step * k, step * (k + 1))
                nc.vector.quantize_mx(
                    out=codes[:, part, :].rearrange("p g c -> p (g c)").bitcast(FP8X4),
                    scales=scales[:, part, :].rearrange("p g c -> p (g c)"),
                    in_=grouped[:, part, :, :].rearrange("p g r t -> p (g r t)"),
                )

        def new_codes():
            codes = code_pool.tile([P, 2, 512], U32, tag="wcodes", align_bytes=64)
            scales = code_pool.tile([P, 2, 512], U8, tag="wscales", align_bytes=64)
            return codes, scales

        x_codes = [const.tile([P, 2, 512], U32, name="x_codes%d" % h, align_bytes=64) for h in range(2)]
        x_scales = [const.tile([P, 2, 512], U8, name="x_scales%d" % h, align_bytes=64) for h in range(2)]

        wides = {}

        def widen(c, s, cast_on_vector):
            if s == 0:
                wide = wbf_pool.tile([P, 4, D], BF16, tag="wbf")
                wides[c] = wide
            cast = cast_pool.tile([P, D], BF16, tag="cast")
            if cast_on_vector:
                nc.vector.tensor_copy(out=cast[:], in_=wq_bytes[c][:, s, :].bitcast(FP8))
            else:
                nc.scalar.copy(out=cast[:], in_=wq_bytes[c][:, s, :].bitcast(FP8))
            for j in range(2):
                cols = slice(512 * j, 512 * (j + 1))
                nc.gpsimd.tensor_tensor(
                    out=wides[c][:, s, cols].rearrange("p (u w e) -> p w u e", u=2, e=2),
                    in0=cast[:, cols].rearrange("p (w u e) -> p w u e", u=2, e=2),
                    in1=sc_bc[:, cols].rearrange("p (w u e) -> p w u e", u=2, e=2),
                    op=ALU.mult,
                )

        def project(h, wcs, j):
            codes, scales = wcs
            accs = []
            for f in range(2):
                acc = psum_mx.tile([P, 512], F32, tag="acc")
                for g in range(2):
                    cols = slice(256 * g + P * f, 256 * g + P * (f + 1))
                    nc.tensor.matmul_mx(
                        out=acc[:],
                        lhsT=codes[:, j, cols].bitcast(FP8X4),
                        lhsT_scale=scales[:, j, cols],
                        rhs=x_codes[h][:, g, :].bitcast(FP8X4),
                        rhs_scale=x_scales[h][:, g, :],
                        start=(g == 0),
                        stop=(g == 1),
                    )
                accs.append(acc)
            return accs

        def product(c, h, j, f, acc):
            term = term_pool.tile([P, 2, 512], F32, tag="term")
            col = 16 * (c // 4) + 8 * f + 2 * (c % 4) + j
            nc.vector.scalar_tensor_tensor(
                out=term[:],
                in0=acc[:].unsqueeze(1).to_broadcast([P, 2, 512]),
                scalar=bias_f[:, col:col + 1],
                in1=table[:, 1 - f:3 - f, h, :],
                op0=ALU.add,
                op1=ALU.mult,
            )
            return term

        def add_pair(engine, terms, j):
            engine.tensor_tensor(out=terms[2 * j][:], in0=terms[2 * j][:], in1=terms[2 * j + 1][:], op=ALU.add)

        def turn_back(terms, rot, j, b, added):
            bank = psum_tp.tile([P, 2, 2, P], F32, tag="tp")
            for a in range(2):
                cols = slice(P * (2 * b + a), P * (2 * b + a + 1))
                for f in range(2):
                    out = bank[:, :, a, HALF * f:HALF * (f + 1)]
                    if added:
                        nc.tensor.transpose(out, terms[2 * j][:, f, cols], ident_f[:])
                    else:
                        for k in range(2):
                            nc.tensor.matmul(
                                out=out,
                                lhsT=terms[2 * j + k][:, f, cols],
                                rhs=ident_f[:],
                                is_transpose=True,
                                start=(k == 0),
                                stop=(k == 1),
                            )
            nc.scalar.copy(out=rot[:, 2 * j:2 * j + 2, 2 * b:2 * b + 2, :], in_=bank[:])

        def store(c, h, rot, heads):
            for sub in range(2):
                nc.sync.dma_start(
                    out=out_views[2 * (c // 4) + sub][
                        :, 2 * (c % 4) + heads.start:2 * (c % 4) + heads.stop, 4 * h:4 * h + 4, :
                    ],
                    in_=rot[:, 2 * heads.start + sub:2 * heads.stop:2, :, :],
                )

        order = [4, 5, 6, 7, 0, 1, 2, 3]
        units = [(c, h) for c in order for h in range(2)]
        groupeds = {}
        wcs = {}

        def rows_of(c):
            return wides[c] if c < 4 else wk_rows[c - 4]

        whole_turns(0)
        parts_of_turns(0)
        whole_turns(1)
        gx0 = new_grouped()
        for s in range(4):
            turn_x(x_half[0], s, gx0)
        quantise(gx0, x_codes[0], x_scales[0])
        g0 = new_grouped()
        for s in range(4):
            turn_w(rows_of(order[0]), s, g0)
        wcs[order[0]] = new_codes()
        quantise(g0, wcs[order[0]][0], wcs[order[0]][1], 2)
        sines(0)
        turn_bias()
        parts_of_turns(1)
        gx1 = new_grouped()
        for s in range(4):
            turn_x(x_half[1], s, gx1)
        sines(1)
        accs = [acc for j in range(2) for acc in project(0, wcs[order[0]], j)]
        terms = [product(order[0], 0, k // 2, k % 2, accs[k]) for k in range(2)]
        quantise(gx1, x_codes[1], x_scales[1])
        terms += [product(order[0], 0, k // 2, k % 2, accs[k]) for k in range(2, 4)]
        groupeds[order[1]] = new_grouped()
        for s in range(4):
            turn_w(rows_of(order[1]), s, groupeds[order[1]])
        waiting = [order[1]]

        jobs = [(order[k], s) for k in range(2, 8) for s in range(4)]
        widen_at_start = {}
        widen_in_middle = {}
        tile_no = 0
        for b in range(11):
            if b % 2 == 1:
                widen_at_start[b] = divmod(tile_no, 4)
                tile_no += 1
            widen_in_middle[b] = divmod(tile_no, 4)
            tile_no += 1

        def prep_job(b, j):
            if 2 * b + j >= len(jobs):
                return
            c, s = jobs[2 * b + j]
            if s == 0:
                groupeds[c] = new_grouped()
            turn_w(rows_of(c), s, groupeds[c], c < 4)
            if s == 3:
                waiting.append(c)

        adders = {n: nc.gpsimd for n in (0, 5, 9, 12, 13, 14)}
        for n in (2, 6, 10):
            adders[n] = nc.vector

        add_pair(adders[0], terms, 0)
        for n in range(16):
            c, h = units[n]
            if n in widen_at_start:
                widen(widen_at_start[n][0], widen_at_start[n][1], True)
            nxt = []
            if n + 1 < 16:
                c2, h2 = units[n + 1]
                accs = [acc for j in range(2) for acc in project(h2, wcs[c2], j)]
                for k in range(4):
                    nxt.append(product(c2, h2, k // 2, k % 2, accs[k]))
                    if k == 1 and waiting:
                        cw = waiting[0]
                        waiting.clear()
                        wcs[cw] = new_codes()
                        quantise(groupeds[cw], wcs[cw][0], wcs[cw][1])
                    if k == 2 and n + 1 in adders:
                        add_pair(adders[n + 1], nxt, 0)
            rot = rot_pool.tile([P, 4, 4, P], F32, tag="rot")
            pairs = [1, 0] if n in adders else [0, 1]
            for k in range(2):
                for f in range(2):
                    turn_back(terms, rot, pairs[k], f, pairs[k] == 0 and n in adders)
                    if k == 0:
                        prep_job(n, f)
                if k == 0 and n in widen_in_middle:
                    widen(widen_in_middle[n][0], widen_in_middle[n][1], False)
                if n == 15:
                    store(c, h, rot, slice(pairs[k], pairs[k] + 1))
            if n < 15:
                store(c, h, rot, slice(0, 2))
            terms = nxt
